import numpy as np
import ml_dtypes


def mxq(x, axis, fmt="e4m3"):
    dtype, down = {"e4m3": (ml_dtypes.float8_e4m3fn, 7), "e5m2": (ml_dtypes.float8_e5m2, 14)}[fmt]
    v = np.moveaxis(np.asarray(x, np.float32).astype(ml_dtypes.bfloat16).astype(np.float64), axis, -1)
    blocks = v.reshape(v.shape[:-1] + (-1, 32))
    amax = np.abs(blocks).max(-1, keepdims=True)
    byte = np.maximum(np.where(amax > 0, np.frexp(amax)[1] - 1 + 127, 0) - down, 1)
    scale = np.exp2(byte - 127.0)
    codes = (blocks / scale).astype(np.float32).astype(dtype).astype(np.float64)
    return np.moveaxis((codes * scale).reshape(v.shape), -1, axis)


WIDE = False


def mx_kscale(k):
    if not WIDE:
        return np.ones(k)
    levels = np.array([10, -10, 5, -5, 0])
    if k % 512:
        return np.exp2(np.random.permutation(np.resize(levels, k // 32))).repeat(32)
    a = np.empty((k // 512, 16))
    for p in range(k // 512):
        a[p, :8] = np.random.permutation(np.resize(levels, 8))
        for g in range(8):
            far = levels[np.abs(levels - a[p, g]) >= 10]
            a[p, g + 8] = far[np.random.randint(len(far))]
    return np.exp2(a.ravel()).repeat(32)


BF16 = ml_dtypes.bfloat16


def bf(x):
    return np.asarray(x, np.float32).astype(BF16)


def f64(x):
    return np.asarray(x).astype(np.float64)


N, C, D, H, W, NHEADS, KSIZE = 1, 1024, 256, 16, 16, 8, 5
PAD = KSIZE // 2
HD = D // NHEADS
WIN = KSIZE * KSIZE


def _patches(t):
    tp = np.pad(t, ((0, 0), (0, 0), (PAD, PAD), (PAD, PAD)))
    return np.stack([tp[:, :, i:i + H, j:j + W] for i in range(KSIZE) for j in range(KSIZE)], axis=2)


def setup_inputs():
    s = mx_kscale(C)
    a = np.sqrt(1.5) / HD ** 0.25
    g = np.concatenate([np.full(2 * D, a), np.ones(D)])
    return {"x": bf(np.random.standard_normal((N, C, H, W)) * s[None, :, None, None]),
            "w_qkv": bf(np.random.standard_normal((3 * D, C)) * g[:, None] / np.sqrt(C) / s[None, :])}


def reference(x, w_qkv):
    xq = mxq(f64(x).reshape(N, C, H * W), 1, "e4m3")
    wq = mxq(f64(w_qkv), 1, "e4m3")
    qkv = (wq @ xq).reshape(N, 3 * D, H, W)
    Q, K, V = np.split(qkv, 3, axis=1)
    Qh = Q.reshape(N, NHEADS, HD, 1, H, W)
    scores = np.sum(_patches(K).reshape(N, NHEADS, HD, WIN, H, W) * Qh, axis=2, keepdims=True)
    e = np.exp(scores - scores.max(axis=3, keepdims=True))
    att = e / e.sum(axis=3, keepdims=True)
    out = np.sum(_patches(V).reshape(N, NHEADS, HD, WIN, H, W) * att, axis=3).reshape(N, D, H, W)
    return out

@@ -1,0 +1,281 @@
+from contextlib import ExitStack
+
+import concourse.mybir as mybir
+from concourse.masks import make_identity
+
+F32 = mybir.dt.float32
+BF16 = mybir.dt.bfloat16
+U32 = mybir.dt.uint32
+U8 = mybir.dt.uint8
+FP8X4 = mybir.dt.float8_e4m3fn_x4
+ALU = mybir.AluOpType
+ACT = mybir.ActivationFunctionType
+AXIS_X = mybir.AxisListType.X
+AXIS_XY = mybir.AxisListType.XY
+
+P = 128
+PACK = 4
+C_IN = 1024
+PASSES = C_IN // (P * PACK)
+D = 256
+HEADS = 8
+HEAD_DIM = D // HEADS
+SIDE = 16
+PIX = SIDE * SIDE
+KSIZE = 5
+PAD = KSIZE // 2
+WIN = KSIZE * KSIZE
+PIX_TILES = PIX // P
+ROWS = P // SIDE
+CH_TILES = D // P
+HALF_HEAD = HEAD_DIM // CH_TILES
+LAST_CUT = 3
+
+FLOPS = 2 * 3 * D * C_IN * PIX + 2 * 2 * D * WIN * PIX
+
+
+def tile_relation_s_kernel(tc, x, w_qkv, out):
+    nc = tc.nc
+    with ExitStack() as ctx:
+        keep = ctx.enter_context(tc.tile_pool(name="keep", bufs=1))
+        small = ctx.enter_context(tc.tile_pool(name="small", bufs=2))
+        work = ctx.enter_context(tc.tile_pool(name="work", bufs=4))
+        stream = ctx.enter_context(tc.psum_pool(name="stream", bufs=4))
+        sums = ctx.enter_context(tc.psum_pool(name="sums", bufs=4))
+
+        x_sb = keep.tile([P, PASSES, PACK, PIX], BF16)
+        nc.sync.dma_start(
+            out=x_sb[:].rearrange("p g t w -> p g (t w)"),
+            in_=x.rearrange("n (g q t) h w -> q (n g) (t h w)", g=PASSES, q=P, t=PACK),
+        )
+        first_row = {"q": 0, "k": D, "v": 2 * D}
+        w_sb = {}
+        for part in ("v", "k", "q"):
+            w_sb[part] = keep.tile([P, CH_TILES, C_IN], BF16, name="w_sb_" + part)
+            for a in range(CH_TILES):
+                row = first_row[part] + a * P
+                nc.sync.dma_start(out=w_sb[part][:, a, :], in_=w_qkv[row : row + P, :])
+
+        ident = keep.tile([P, P], F32)
+        make_identity(nc, ident[:])
+        split_heads = keep.tile([P, P], F32)
+        nc.vector.tensor_copy(
+            out=split_heads[:].rearrange("p (b h c) -> p b h c", b=CH_TILES, c=HALF_HEAD),
+            in_=ident[:].rearrange("p (h b c) -> p b h c", b=CH_TILES, c=HALF_HEAD),
+        )
+        k_pad = keep.tile([P, CH_TILES, SIDE + 2 * PAD, SIDE + 2 * PAD], F32)
+        nc.vector.memset(k_pad[:], 0.0)
+        v_win = keep.tile([P, PIX_TILES, WIN, D], F32)
+        centre = WIN // 2
+        zero = keep.tile([P, 1], F32)
+        nc.vector.memset(zero[:], 0.0)
+        nc.scalar.copy(
+            out=v_win[0 : P // 2, 0, 0:centre, :],
+            in_=zero[0 : P // 2].unsqueeze(2).to_broadcast([P // 2, centre, D]),
+        )
+        nc.gpsimd.memset(v_win[P // 2 : P, PIX_TILES - 1, centre + 1 : WIN, :], 0.0)
+        inside = keep.tile([P, KSIZE], F32)
+        for j in range(KSIZE):
+            lo = max(0, PAD - j)
+            hi = SIDE - max(0, j - PAD)
+            nc.vector.tensor_reduce(
+                out=inside[:, j : j + 1],
+                in_=ident[:].rearrange("p (y x) -> p y x", x=SIDE)[:, :, lo:hi],
+                axis=AXIS_XY,
+                op=ALU.add,
+            )
+        warm_out = keep.tile([P, 1], F32)
+        nc.scalar.activation(out=warm_out[:], in_=zero[:], func=ACT.Exp)
+
+        x_grouped = keep.tile([P, PASSES, PIX, PACK], BF16, align_bytes=64)
+        nc.vector.tensor_copy(out=x_grouped[:], in_=x_sb[:].rearrange("p g t w -> p g w t"))
+        x_codes = keep.tile([P, PASSES, PIX], U32, align_bytes=64)
+        x_scales = keep.tile([P, PASSES, PIX], U8, align_bytes=64)
+        nc.vector.quantize_mx(
+            out=x_codes[:].rearrange("p g w -> p (g w)").bitcast(FP8X4),
+            scales=x_scales[:].rearrange("p g w -> p (g w)"),
+            in_=x_grouped[:].rearrange("p g w t -> p (g w t)"),
+        )
+
+        def quantise_weight(part, split):
+            w_grouped = keep.tile([P, PASSES * D * PACK], BF16, align_bytes=64, name="w_grouped_" + part)
+            w_words = w_grouped[:].bitcast(F32)
+            for a in range(CH_TILES):
+                wt = stream.tile([P, PASSES, 2, P], F32, tag="stream")
+                words = w_sb[part][:, a, :].bitcast(F32)
+                order = split_heads if split else ident
+                for g in range(PASSES):
+                    for u in range(2):
+                        nc.tensor.transpose(
+                            wt[:, g, u, :], words[:, 2 * P * g + u : 2 * P * (g + 1) : 2], order[:]
+                        )
+                copy_out = nc.vector.tensor_copy if a == 0 else nc.scalar.copy
+                for g in range(PASSES):
+                    if split:
+                        n = P // CH_TILES
+                        copy_out(
+                            out=w_words.rearrange("p (b g o u) -> p b g o u", b=CH_TILES, g=PASSES, u=2)[
+                                :, :, g, a * n : (a + 1) * n, :
+                            ],
+                            in_=wt[:, g].rearrange("p u (b o) -> p b o u", b=CH_TILES),
+                        )
+                    else:
+                        copy_out(
+                            out=w_words.rearrange("p (g o u) -> p g o u", g=PASSES, u=2)[:, g, a * P : (a + 1) * P, :],
+                            in_=wt[:, g].rearrange("p u o -> p o u"),
+                        )
+            w_codes = keep.tile([P, PASSES * D], U32, align_bytes=64, name="w_codes_" + part)
+            w_scales = keep.tile([P, PASSES * D], U8, align_bytes=64, name="w_scales_" + part)
+            nc.vector.quantize_mx(out=w_codes[:].bitcast(FP8X4), scales=w_scales[:], in_=w_grouped[:])
+            if split:
+                shape = "p (b g o) -> p b g o"
+                return (
+                    w_codes[:].rearrange(shape, b=CH_TILES, g=PASSES),
+                    w_scales[:].rearrange(shape, b=CH_TILES, g=PASSES),
+                )
+            return w_codes[:].rearrange("p (g o) -> p g o", g=PASSES), w_scales[:].rearrange("p (g o) -> p g o", g=PASSES)
+
+        parked = out.rearrange("n c h w -> (n c) (h w)")
+        v_codes, v_scales = quantise_weight("v", False)
+        v_sb = keep.tile([P, PIX_TILES, D], F32)
+        for t in range(PIX_TILES):
+            v_psum = sums.tile([P, D], F32, tag="sums")
+            cols = slice(t * P, (t + 1) * P)
+            for g in range(PASSES):
+                nc.tensor.matmul_mx(
+                    out=v_psum[:],
+                    lhsT=x_codes[:, g, cols].bitcast(FP8X4),
+                    lhsT_scale=x_scales[:, g, cols],
+                    rhs=v_codes[:, g, :].bitcast(FP8X4),
+                    rhs_scale=v_scales[:, g, :],
+                    start=(g == 0),
+                    stop=(g == PASSES - 1),
+                )
+            nc.scalar.copy(out=v_sb[:, t, :], in_=v_psum[:])
+        nc.sync.dma_start(out=parked.rearrange("(t p) c -> p t c", p=P), in_=v_sb[:])
+
+        for t in range(PIX_TILES):
+            for o in range(WIN):
+                i, j = divmod(o, KSIZE)
+                top_row = t * ROWS + i - PAD
+                first = top_row * SIDE + j - PAD
+                lo = max(0, -top_row) * SIDE
+                hi = min(ROWS, SIDE - top_row) * SIDE
+                pieces = [(lo, hi)]
+                if first + lo < 0:
+                    pieces = [(-first, lo + SIDE), (lo + SIDE, hi)]
+                if first + hi > PIX:
+                    pieces = [(lo, hi - SIDE), (hi - SIDE, PIX - first)]
+                for p_lo, p_hi in pieces:
+                    nc.sync.dma_start(out=v_win[p_lo:p_hi, t, o, :], in_=parked[first + p_lo : first + p_hi, :])
+
+        def project_channels_first(part):
+            w_codes, w_scales = quantise_weight(part, True)
+            projected = sums.tile([P, CH_TILES, PIX], F32, tag="sums", name="projected_" + part)
+            for b in range(CH_TILES):
+                for g in range(PASSES):
+                    nc.tensor.matmul_mx(
+                        out=projected[:, b, :],
+                        lhsT=w_codes[:, b, g, :].bitcast(FP8X4),
+                        lhsT_scale=w_scales[:, b, g, :],
+                        rhs=x_codes[:, g, :].bitcast(FP8X4),
+                        rhs_scale=x_scales[:, g, :],
+                        start=(g == 0),
+                        stop=(g == PASSES - 1),
+                    )
+            return projected[:].rearrange("p b (y x) -> p b y x", x=SIDE)
+
+        nc.scalar.copy(out=k_pad[:, :, PAD : PAD + SIDE, PAD : PAD + SIDE], in_=project_channels_first("k"))
+        q_psum = project_channels_first("q")
+        q_sb = keep.tile([P, CH_TILES, SIDE, SIDE], F32)
+        nc.vector.tensor_copy(out=q_sb[:], in_=q_psum)
+
+        rows_of_softmax = PIX_TILES * HEADS
+        scores = keep.tile([P, WIN, rows_of_softmax], F32)
+        for o_first in range(0, WIN, 2):
+            n = min(2, WIN - o_first)
+            halves = stream.tile([P, 2, PIX_TILES, P], F32, tag="stream")
+            for oo in range(n):
+                i, j = divmod(o_first + oo, KSIZE)
+                k_window = k_pad[:, :, i : i + SIDE, j : j + SIDE]
+                qk = work.tile([P, CH_TILES, PIX], F32, bufs=8)
+                qk_image = qk[:].rearrange("p b (y x) -> p b y x", x=SIDE)
+                if oo == 0:
+                    nc.vector.tensor_tensor(out=qk_image, in0=q_psum, in1=k_window, op=ALU.mult)
+                else:
+                    nc.gpsimd.tensor_tensor(out=qk_image, in0=q_sb[:], in1=k_window, op=ALU.mult)
+                for t in range(PIX_TILES):
+                    for b in range(CH_TILES):
+                        nc.tensor.matmul(
+                            out=halves[:, oo, t, :],
+                            lhsT=qk[:, b, t * P : (t + 1) * P],
+                            rhs=ident[:],
+                            is_transpose=True,
+                            start=(b == 0),
+                            stop=(b == CH_TILES - 1),
+                        )
+            nc.vector.tensor_reduce(
+                out=scores[:, o_first : o_first + n, :].rearrange("p o r -> p (o r)"),
+                in_=halves[:, 0:n].rearrange("p o t (h c) -> p (o t h) c", c=HALF_HEAD),
+                axis=AXIS_X,
+                op=ALU.add,
+            )
+
+        top = small.tile([P, rows_of_softmax], F32)
+        nc.vector.tensor_reduce(out=top[:], in_=scores[:].rearrange("p o r -> p r o"), axis=AXIS_X, op=ALU.max)
+        centred = keep.tile([P, WIN, rows_of_softmax], F32)
+        nc.vector.tensor_tensor(
+            out=centred[:],
+            in0=scores[:],
+            in1=top[:].unsqueeze(1).to_broadcast([P, WIN, rows_of_softmax]),
+            op=ALU.subtract,
+        )
+        e = keep.tile([P, WIN, rows_of_softmax], F32)
+        nc.scalar.activation(out=e[:], in_=centred[:], func=ACT.Exp)
+        total = small.tile([P, rows_of_softmax], F32)
+        nc.vector.tensor_reduce(out=total[:], in_=e[:].rearrange("p o r -> p r o"), axis=AXIS_X, op=ALU.add)
+        inv = small.tile([P, rows_of_softmax], F32)
+        nc.vector.reciprocal(out=inv[:], in_=total[:])
+        inv_inside = small.tile([P, KSIZE, rows_of_softmax], F32)
+        nc.vector.tensor_tensor(
+            out=inv_inside[:],
+            in0=inv[:].unsqueeze(1).to_broadcast([P, KSIZE, rows_of_softmax]),
+            in1=inside[:].unsqueeze(2).to_broadcast([P, KSIZE, rows_of_softmax]),
+            op=ALU.mult,
+        )
+        att = keep.tile([P, WIN, PIX_TILES, HEADS], F32)
+        nc.vector.tensor_tensor(
+            out=att[:].rearrange("p (i j) t h -> p i (j t h)", j=KSIZE),
+            in0=e[:].rearrange("p (i j) r -> p i (j r)", j=KSIZE),
+            in1=inv_inside[:].rearrange("p j r -> p (j r)").unsqueeze(1).to_broadcast([P, KSIZE, KSIZE * rows_of_softmax]),
+            op=ALU.mult,
+        )
+
+        out_view = out.rearrange("n (ct c) h w -> c (n ct) (h w)", ct=CH_TILES, c=P)
+        for t in range(PIX_TILES):
+            result = [sums.tile([P, P], F32, tag="sums", name="result_%d" % ct) for ct in range(CH_TILES)]
+            chunks = [(o, KSIZE) for o in range(0, WIN, KSIZE)]
+            if t == PIX_TILES - 1:
+                chunks[-1:] = [(WIN - KSIZE, LAST_CUT), (WIN - KSIZE + LAST_CUT, KSIZE - LAST_CUT)]
+            for o_first, n in chunks:
+                av = work.tile([P, KSIZE, D], F32)
+                nc.vector.tensor_tensor(
+                    out=av[:, 0:n, :].rearrange("p o (h c) -> p o h c", h=HEADS),
+                    in0=v_win[:, t, o_first : o_first + n, :].rearrange("p o (h c) -> p o h c", h=HEADS),
+                    in1=att[:, o_first : o_first + n, t, :].unsqueeze(3).to_broadcast([P, n, HEADS, HEAD_DIM]),
+                    op=ALU.mult,
+                )
+                for oo in range(n):
+                    for ct in range(CH_TILES):
+                        nc.tensor.matmul(
+                            out=result[ct][:],
+                            lhsT=av[:, oo, ct * P : (ct + 1) * P],
+                            rhs=ident[:],
+                            is_transpose=True,
+                            start=(o_first + oo == 0),
+                            stop=(o_first + oo == WIN - 1),
+                        )
+            out_sb = small.tile([P, CH_TILES, P], F32)
+            for ct in range(CH_TILES):
+                nc.scalar.copy(out=out_sb[:, ct, :], in_=result[ct][:])
+            nc.sync.dma_start(out=out_view[:, :, t * P : (t + 1) * P], in_=out_sb[:])

@@ -6,6 +6,7 @@ from concourse.masks import make_identity
 F32 = mybir.dt.float32
 BF16 = mybir.dt.bfloat16
 U32 = mybir.dt.uint32
+I32 = mybir.dt.int32
 U8 = mybir.dt.uint8
 FP8X4 = mybir.dt.float8_e4m3fn_x4
 ALU = mybir.AluOpType
@@ -27,9 +28,22 @@ PAD = KSIZE // 2
 WIN = KSIZE * KSIZE
 PIX_TILES = PIX // P
 ROWS = P // SIDE
-CH_TILES = D // P
-HALF_HEAD = HEAD_DIM // CH_TILES
-LAST_CUT = 3
+GROUP = 4
+HALVES = 2
+HALF_HEAD = HEAD_DIM // HALVES
+HALF = GROUP * HALF_HEAD
+
+BLOCKS = 8
+BLOCK_PIX = PIX // BLOCKS
+NB_ROWS = 2 + 2 * PAD
+NB = NB_ROWS * SIDE
+BESIDE = 2 * KSIZE
+COLS = NB + BESIDE
+SUM_TILES = ((0, 3, 0), (3, 2, 4), (5, 3, 8))
+BIG = 2.0**100
+
+SCALAR_FROM = (3, 4, 3, 4, 3)
+GPSIMD_OFFSETS = tuple(range(1, WIN, 2))
 
 FLOPS = 2 * 3 * D * C_IN * PIX + 2 * 2 * D * WIN * PIX
 
@@ -38,244 +52,512 @@ def tile_relation_s_kernel(tc, x, w_qkv, out):
     nc = tc.nc
     with ExitStack() as ctx:
         keep = ctx.enter_context(tc.tile_pool(name="keep", bufs=1))
-        small = ctx.enter_context(tc.tile_pool(name="small", bufs=2))
         work = ctx.enter_context(tc.tile_pool(name="work", bufs=4))
-        stream = ctx.enter_context(tc.psum_pool(name="stream", bufs=4))
-        sums = ctx.enter_context(tc.psum_pool(name="sums", bufs=4))
+        stream = ctx.enter_context(tc.psum_pool(name="stream", bufs=3))
+        misc = ctx.enter_context(tc.psum_pool(name="misc", bufs=4))
+        hold = ctx.enter_context(tc.psum_pool(name="hold", bufs=1))
+        ctx.enter_context(tc.manual_schedule())
 
         x_sb = keep.tile([P, PASSES, PACK, PIX], BF16)
-        nc.sync.dma_start(
-            out=x_sb[:].rearrange("p g t w -> p g (t w)"),
-            in_=x.rearrange("n (g q t) h w -> q (n g) (t h w)", g=PASSES, q=P, t=PACK),
-        )
-        first_row = {"q": 0, "k": D, "v": 2 * D}
+        x_view = x.rearrange("n (g q t) h w -> q (n g) (t h w)", g=PASSES, q=P, t=PACK)
+        for g in range(PASSES):
+            nc.sync.dma_start(out=x_sb[:, g].rearrange("p t w -> p (t w)"), in_=x_view[:, g, :])
+        first_row = {"qa": 0, "qb": P, "ka": D, "kb": D + P, "va": 2 * D, "vb": 2 * D + P}
         w_sb = {}
-        for part in ("v", "k", "q"):
-            w_sb[part] = keep.tile([P, CH_TILES, C_IN], BF16, name="w_sb_" + part)
-            for a in range(CH_TILES):
-                row = first_row[part] + a * P
-                nc.sync.dma_start(out=w_sb[part][:, a, :], in_=w_qkv[row : row + P, :])
+        for part in ("kb", "qb", "vb", "qa", "ka", "va"):
+            w_sb[part] = keep.tile([P, C_IN], BF16, name="w_sb_" + part)
+            row = first_row[part]
+            nc.sync.dma_start(out=w_sb[part][:], in_=w_qkv[row : row + P, :])
 
         ident = keep.tile([P, P], F32)
         make_identity(nc, ident[:])
+        zero = keep.tile([P, P], F32)
+        nc.vector.memset(zero[:], 0.0)
+        warm_out = keep.tile([P, 1], F32)
+        nc.scalar.activation(out=warm_out[:], in_=zero[:, 0:1], func=ACT.Exp)
+        parked = out.rearrange("n c h w -> (n c) (h w)").rearrange("r (s c) -> (r s) c", s=2)
+        nc.scalar.dma_start(out=parked[0:P, :], in_=zero[:])
+        nc.scalar.dma_start(out=parked[3 * P : 4 * P, :], in_=zero[:])
+        q_diag = keep.tile([P, BLOCKS, GROUP, BLOCK_PIX], F32)
+        nc.scalar.copy(
+            out=q_diag[:].rearrange("p k h w -> p (k h w)"), in_=zero[:, 0:1].to_broadcast([P, BLOCKS * P])
+        )
+        k_pad = keep.tile([P, HALVES, ROWS + 2 * PAD, SIDE + 2 * PAD], F32)
+        nc.vector.memset(k_pad[:], 0.0)
+        split_codes = {}
+        split_scales = {}
+        for part in ("kb", "qb"):
+            split_codes[part] = keep.tile([P, PASSES, 5 * HALF], U32, align_bytes=64, name="codes_" + part)
+            split_scales[part] = keep.tile([P, PASSES, 5 * HALF], U8, align_bytes=64, name="scales_" + part)
+            nc.vector.memset(split_codes[part][:].rearrange("p g (z o) -> p g z o", o=HALF)[:, :, 0:5:2, :], 0)
+            nc.vector.memset(split_scales[part][:].rearrange("p g o -> p (g o)").bitcast(I32), 0)
+        ka_pad = keep.tile([P, SIDE + 2 * PAD, SIDE], F32)
+        nc.gpsimd.memset(ka_pad[:], 0.0)
+        column = keep.tile([P, SIDE + 2 * PAD], F32)
+        nc.gpsimd.memset(column[:], 0.0)
+        att_a = keep.tile([P, BLOCKS, P], F32)
+        nc.gpsimd.memset(att_a[:], 0.0)
+        att_t = keep.tile([P, BLOCKS * P + P], F32)
+        nc.gpsimd.memset(att_t[:, BLOCKS * P : BLOCKS * P + P], 0.0)
         split_heads = keep.tile([P, P], F32)
         nc.vector.tensor_copy(
-            out=split_heads[:].rearrange("p (b h c) -> p b h c", b=CH_TILES, c=HALF_HEAD),
-            in_=ident[:].rearrange("p (h b c) -> p b h c", b=CH_TILES, c=HALF_HEAD),
+            out=split_heads[:].rearrange("p (b h c) -> p b h c", b=HALVES, c=HALF_HEAD),
+            in_=ident[:].rearrange("p (h b c) -> p b h c", b=HALVES, c=HALF_HEAD),
         )
-        k_pad = keep.tile([P, CH_TILES, SIDE + 2 * PAD, SIDE + 2 * PAD], F32)
-        nc.vector.memset(k_pad[:], 0.0)
-        v_win = keep.tile([P, PIX_TILES, WIN, D], F32)
-        centre = WIN // 2
-        zero = keep.tile([P, 1], F32)
-        nc.vector.memset(zero[:], 0.0)
-        nc.scalar.copy(
-            out=v_win[0 : P // 2, 0, 0:centre, :],
-            in_=zero[0 : P // 2].unsqueeze(2).to_broadcast([P // 2, centre, D]),
+        nc.vector.tensor_reduce(
+            out=column[:, PAD : PAD + SIDE],
+            in_=ident[:].rearrange("p (y x) -> p x y", x=SIDE),
+            axis=AXIS_X,
+            op=ALU.add,
         )
-        nc.gpsimd.memset(v_win[P // 2 : P, PIX_TILES - 1, centre + 1 : WIN, :], 0.0)
+        row_of_two = keep.tile([P, 2], F32)
+        nc.vector.tensor_reduce(
+            out=row_of_two[:],
+            in_=ident[:].rearrange("p (y r x) -> p r y x", r=2, x=SIDE),
+            axis=AXIS_XY,
+            op=ALU.add,
+        )
         inside = keep.tile([P, KSIZE], F32)
         for j in range(KSIZE):
-            lo = max(0, PAD - j)
-            hi = SIDE - max(0, j - PAD)
-            nc.vector.tensor_reduce(
-                out=inside[:, j : j + 1],
-                in_=ident[:].rearrange("p (y x) -> p y x", x=SIDE)[:, :, lo:hi],
-                axis=AXIS_XY,
-                op=ALU.add,
+            lo = PAD + max(0, PAD - j)
+            hi = PAD + SIDE - max(0, j - PAD)
+            nc.vector.tensor_reduce(out=inside[:, j : j + 1], in_=column[:, lo:hi], axis=AXIS_X, op=ALU.add)
+        band = keep.tile([P, KSIZE - 1, SIDE], F32)
+        nc.gpsimd.tensor_tensor(out=band[:, 0], in0=column[:, 0:SIDE], in1=column[:, 1 : 1 + SIDE], op=ALU.add)
+        for j in range(2, KSIZE):
+            nc.gpsimd.tensor_tensor(out=band[:, j - 1], in0=band[:, j - 2], in1=column[:, j : j + SIDE], op=ALU.add)
+        in_window = keep.tile([P, NB_ROWS, SIDE], F32)
+        for rows, pick in ((slice(0, 1), row_of_two[:, 0:1]), (slice(1, 5), 1.0), (slice(5, 6), row_of_two[:, 1:2])):
+            n = rows.stop - rows.start
+            nc.gpsimd.tensor_scalar(
+                out=in_window[:, rows],
+                in0=band[:, KSIZE - 2].unsqueeze(1).to_broadcast([P, n, SIDE]),
+                scalar1=pick,
+                scalar2=0.0,
+                op0=ALU.mult,
+                op1=ALU.add,
             )
-        warm_out = keep.tile([P, 1], F32)
-        nc.scalar.activation(out=warm_out[:], in_=zero[:], func=ACT.Exp)
+        mask = keep.tile([P, NB], F32)
+        nc.gpsimd.tensor_scalar(
+            out=mask[:],
+            in0=in_window[:].rearrange("p r x -> p (r x)"),
+            scalar1=1.0,
+            scalar2=BIG,
+            op0=ALU.subtract,
+            op1=ALU.mult,
+        )
+        beside = keep.tile([P, 2], F32)
+        nc.gpsimd.tensor_tensor(out=beside[:, 0:1], in0=inside[:, 0:1], in1=inside[:, 4:5], op=ALU.add)
+        nc.gpsimd.tensor_tensor(out=beside[:, 1:2], in0=inside[:, 1:2], in1=inside[:, 3:4], op=ALU.add)
+        masked = keep.tile([P, BLOCKS, COLS], F32)
+        for f in range(2):
+            nc.gpsimd.tensor_scalar(
+                out=masked[:, :, NB + f * KSIZE : NB + (f + 1) * KSIZE],
+                in0=beside[:, f : f + 1].unsqueeze(1).to_broadcast([P, BLOCKS, KSIZE]),
+                scalar1=-BIG,
+                scalar2=BIG,
+                op0=ALU.mult,
+                op1=ALU.add,
+            )
 
         x_grouped = keep.tile([P, PASSES, PIX, PACK], BF16, align_bytes=64)
-        nc.vector.tensor_copy(out=x_grouped[:], in_=x_sb[:].rearrange("p g t w -> p g w t"))
         x_codes = keep.tile([P, PASSES, PIX], U32, align_bytes=64)
         x_scales = keep.tile([P, PASSES, PIX], U8, align_bytes=64)
-        nc.vector.quantize_mx(
-            out=x_codes[:].rearrange("p g w -> p (g w)").bitcast(FP8X4),
-            scales=x_scales[:].rearrange("p g w -> p (g w)"),
-            in_=x_grouped[:].rearrange("p g w t -> p (g w t)"),
-        )
+        for g in range(PASSES):
+            nc.vector.tensor_copy(out=x_grouped[:, g], in_=x_sb[:, g].rearrange("p t w -> p w t"))
+        for g in range(PASSES):
+            nc.vector.quantize_mx(
+                out=x_codes[:, g].bitcast(FP8X4),
+                scales=x_scales[:, g],
+                in_=x_grouped[:, g].rearrange("p w t -> p (w t)"),
+            )
+        x_mx = (x_codes, x_scales)
 
-        def quantise_weight(part, split):
-            w_grouped = keep.tile([P, PASSES * D * PACK], BF16, align_bytes=64, name="w_grouped_" + part)
-            w_words = w_grouped[:].bitcast(F32)
-            for a in range(CH_TILES):
-                wt = stream.tile([P, PASSES, 2, P], F32, tag="stream")
-                words = w_sb[part][:, a, :].bitcast(F32)
-                order = split_heads if split else ident
-                for g in range(PASSES):
-                    for u in range(2):
-                        nc.tensor.transpose(
-                            wt[:, g, u, :], words[:, 2 * P * g + u : 2 * P * (g + 1) : 2], order[:]
-                        )
-                copy_out = nc.vector.tensor_copy if a == 0 else nc.scalar.copy
-                for g in range(PASSES):
-                    if split:
-                        n = P // CH_TILES
-                        copy_out(
-                            out=w_words.rearrange("p (b g o u) -> p b g o u", b=CH_TILES, g=PASSES, u=2)[
-                                :, :, g, a * n : (a + 1) * n, :
-                            ],
-                            in_=wt[:, g].rearrange("p u (b o) -> p b o u", b=CH_TILES),
-                        )
-                    else:
-                        copy_out(
-                            out=w_words.rearrange("p (g o u) -> p g o u", g=PASSES, u=2)[:, g, a * P : (a + 1) * P, :],
-                            in_=wt[:, g].rearrange("p u o -> p o u"),
-                        )
-            w_codes = keep.tile([P, PASSES * D], U32, align_bytes=64, name="w_codes_" + part)
-            w_scales = keep.tile([P, PASSES * D], U8, align_bytes=64, name="w_scales_" + part)
-            nc.vector.quantize_mx(out=w_codes[:].bitcast(FP8X4), scales=w_scales[:], in_=w_grouped[:])
-            if split:
-                shape = "p (b g o) -> p b g o"
-                return (
-                    w_codes[:].rearrange(shape, b=CH_TILES, g=PASSES),
-                    w_scales[:].rearrange(shape, b=CH_TILES, g=PASSES),
-                )
-            return w_codes[:].rearrange("p (g o) -> p g o", g=PASSES), w_scales[:].rearrange("p (g o) -> p g o", g=PASSES)
+        def transpose_weight(part, order):
+            words = w_sb[part][:].bitcast(F32)
+            wt = stream.tile([P, PASSES, 2, P], F32, tag="stream", name="wt_" + part)
+            for g in range(PASSES):
+                for u in range(2):
+                    nc.tensor.transpose(wt[:, g, u, :], words[:, 2 * P * g + u : 2 * P * (g + 1) : 2], order[:])
+            return wt
 
-        parked = out.rearrange("n c h w -> (n c) (h w)")
-        v_codes, v_scales = quantise_weight("v", False)
-        v_sb = keep.tile([P, PIX_TILES, D], F32)
-        for t in range(PIX_TILES):
-            v_psum = sums.tile([P, D], F32, tag="sums")
-            cols = slice(t * P, (t + 1) * P)
+        def group_weight(part, wt, copy_out):
+            grouped = keep.tile([P, PASSES, P, PACK], BF16, align_bytes=64, name="grouped_" + part)
+            copy_out(
+                out=grouped[:].rearrange("p g o t -> p (g o t)").bitcast(F32).rearrange("p (g o u) -> p g o u", g=PASSES, u=2),
+                in_=wt[:].rearrange("p g u o -> p g o u"),
+            )
+            return grouped
+
+        def quantise_weight(part, grouped):
+            codes = keep.tile([P, PASSES, P], U32, align_bytes=64, name="codes_" + part)
+            scales = keep.tile([P, PASSES, P], U8, align_bytes=64, name="scales_" + part)
+            nc.vector.quantize_mx(
+                out=codes[:].rearrange("p g o -> p (g o)").bitcast(FP8X4),
+                scales=scales[:].rearrange("p g o -> p (g o)"),
+                in_=grouped[:].rearrange("p g o t -> p (g o t)"),
+            )
+            return codes, scales
+
+        def quantise_split_weight(part, grouped):
+            for g in range(PASSES):
+                for b in range(HALVES):
+                    to = slice(HALF + 2 * HALF * b, 2 * HALF + 2 * HALF * b)
+                    nc.vector.quantize_mx(
+                        out=split_codes[part][:, g, to].bitcast(FP8X4),
+                        scales=split_scales[part][:, g, to],
+                        in_=grouped[:, g, b * HALF : (b + 1) * HALF, :].rearrange("p o t -> p (o t)"),
+                    )
+            return split_codes[part], split_scales[part]
+
+        def mx(out_ap, lhs, lhs_cols, rhs, rhs_cols, first=True, last=True):
             for g in range(PASSES):
                 nc.tensor.matmul_mx(
-                    out=v_psum[:],
-                    lhsT=x_codes[:, g, cols].bitcast(FP8X4),
-                    lhsT_scale=x_scales[:, g, cols],
-                    rhs=v_codes[:, g, :].bitcast(FP8X4),
-                    rhs_scale=v_scales[:, g, :],
-                    start=(g == 0),
-                    stop=(g == PASSES - 1),
+                    out=out_ap,
+                    lhsT=lhs[0][:, g, lhs_cols].bitcast(FP8X4),
+                    lhsT_scale=lhs[1][:, g, lhs_cols],
+                    rhs=rhs[0][:, g, rhs_cols].bitcast(FP8X4),
+                    rhs_scale=rhs[1][:, g, rhs_cols],
+                    start=(first and g == 0),
+                    stop=(last and g == PASSES - 1),
                 )
-            nc.scalar.copy(out=v_sb[:, t, :], in_=v_psum[:])
-        nc.sync.dma_start(out=parked.rearrange("(t p) c -> p t c", p=P), in_=v_sb[:])
 
+        def mx_split(out_ap, part, b, other):
+            for t in range(PIX_TILES):
+                start = HALF + 2 * HALF * b - HALF * t
+                tile = (t + other) % PIX_TILES
+                mx(
+                    out_ap,
+                    part,
+                    slice(start, start + P),
+                    x_mx,
+                    slice(tile * P, (tile + 1) * P),
+                    first=(t == 0),
+                    last=(t == PIX_TILES - 1),
+                )
+
+        every = slice(0, P)
+        all_pix = slice(0, PIX)
+        to_vector = nc.vector.tensor_copy
+        to_scalar = nc.scalar.copy
+
+        wt_kb = transpose_weight("kb", split_heads)
+        wt_qb = transpose_weight("qb", split_heads)
+        wt_vb = transpose_weight("vb", ident)
+        kb_mx = quantise_split_weight("kb", group_weight("kb", wt_kb, to_vector))
+        qb_mx = quantise_split_weight("qb", group_weight("qb", wt_qb, to_scalar))
+        vb_grouped = group_weight("vb", wt_vb, to_scalar)
+        vb_mx = quantise_weight("vb", vb_grouped)
+        kb_psum = misc.tile([P, 2, HALVES, P], F32, tag="misc")
+        for b in range(HALVES):
+            mx_split(kb_psum[:, 0, b, :], kb_mx, b, 0)
+        qb_psum = hold.tile([P, HALVES, P], F32)
+        for b in range(HALVES):
+            mx_split(qb_psum[:, b, :], qb_mx, b, 0)
+        for b in range(HALVES):
+            mx_split(kb_psum[:, 1, b, :], kb_mx, b, 1)
+        kb_view = kb_psum[:].rearrange("p o b (y x) -> p o b y x", x=SIDE)
+        inner = slice(PAD, PAD + SIDE)
+        qb_sb = keep.tile([P, HALVES, P], F32)
+        nc.scalar.copy(out=qb_sb[:], in_=qb_psum[:])
+        nc.vector.tensor_copy(out=k_pad[:, :, PAD : PAD + ROWS, inner], in_=kb_view[:, 0])
+        nc.scalar.copy(
+            out=k_pad[0:HALF, :, PAD + ROWS : 2 * PAD + ROWS, inner], in_=kb_view[0:HALF, 1, :, 0:PAD, :]
+        )
+        nc.vector.tensor_copy(out=k_pad[HALF:P, :, 0:PAD, inner], in_=kb_view[HALF:P, 1, :, ROWS - PAD : ROWS, :])
+
+        vb_psum = misc.tile([P, PIX_TILES, P], F32, tag="misc")
         for t in range(PIX_TILES):
-            for o in range(WIN):
-                i, j = divmod(o, KSIZE)
-                top_row = t * ROWS + i - PAD
-                first = top_row * SIDE + j - PAD
-                lo = max(0, -top_row) * SIDE
-                hi = min(ROWS, SIDE - top_row) * SIDE
-                pieces = [(lo, hi)]
-                if first + lo < 0:
-                    pieces = [(-first, lo + SIDE), (lo + SIDE, hi)]
-                if first + hi > PIX:
-                    pieces = [(lo, hi - SIDE), (hi - SIDE, PIX - first)]
-                for p_lo, p_hi in pieces:
-                    nc.sync.dma_start(out=v_win[p_lo:p_hi, t, o, :], in_=parked[first + p_lo : first + p_hi, :])
+            mx(vb_psum[:, t, :], x_mx, slice(t * P, (t + 1) * P), vb_mx, every)
+        vb_sb = keep.tile([P, PIX_TILES, P], F32)
+        nc.scalar.copy(out=vb_sb[:], in_=vb_psum[:])
+        nc.sync.dma_start(out=parked[P : 3 * P, :].rearrange("(t p) c -> p t c", p=P), in_=vb_sb[:])
+        v_win = keep.tile([P, PIX_TILES, WIN, P], F32)
+        for o in range(WIN):
+            i, j = divmod(o, KSIZE)
+            first = P + (i - PAD) * SIDE + j - PAD
+            nc.sync.dma_start(
+                out=v_win[:, :, o, :], in_=parked[first : first + PIX, :].rearrange("(t p) c -> p t c", p=P)
+            )
 
-        def project_channels_first(part):
-            w_codes, w_scales = quantise_weight(part, True)
-            projected = sums.tile([P, CH_TILES, PIX], F32, tag="sums", name="projected_" + part)
-            for b in range(CH_TILES):
-                for g in range(PASSES):
-                    nc.tensor.matmul_mx(
-                        out=projected[:, b, :],
-                        lhsT=w_codes[:, b, g, :].bitcast(FP8X4),
-                        lhsT_scale=w_scales[:, b, g, :],
-                        rhs=x_codes[:, g, :].bitcast(FP8X4),
-                        rhs_scale=x_scales[:, g, :],
-                        start=(g == 0),
-                        stop=(g == PASSES - 1),
+
+        a_mx = {}
+
+        def a_weight(part):
+            a_mx[part] = quantise_weight(part, group_weight(part, wt_a[part], to_scalar))
+
+        qka_psum = misc.tile([P, 2, PIX], F32, tag="misc")
+        va_psum = misc.tile([P, len(SUM_TILES), P], F32, tag="misc")
+        va_sb = keep.tile([P, len(SUM_TILES), P], F32)
+        top_a = keep.tile([P, BLOCKS], F32)
+        minus_top = keep.tile([P, BLOCKS], F32)
+        e_a = keep.tile([P, BLOCKS, COLS], F32)
+        total_a = keep.tile([P, BLOCKS], F32)
+        inv_a = keep.tile([P, BLOCKS], F32)
+
+        def a_project():
+            mx(qka_psum[:, 0, :], a_mx["qa"], every, x_mx, all_pix)
+            mx(qka_psum[:, 1, :], a_mx["ka"], every, x_mx, all_pix)
+            nc.scalar.copy(
+                out=ka_pad[:, PAD : PAD + SIDE, :], in_=qka_psum[:, 1, :].rearrange("p (y x) -> p y x", x=SIDE)
+            )
+            for h in range(GROUP):
+                rows = slice(h * HEAD_DIM, (h + 1) * HEAD_DIM)
+                nc.scalar.copy(
+                    out=q_diag[rows, :, h, :], in_=qka_psum[rows, 0, :].rearrange("p (k w) -> p k w", k=BLOCKS)
+                )
+
+        def a_values():
+            for s, (block, blocks, top) in enumerate(SUM_TILES):
+                mx(va_psum[:, s, :], x_mx, slice(top * SIDE, top * SIDE + P), a_mx["va"], every)
+            nc.scalar.copy(out=va_sb[:], in_=va_psum[:])
+
+        def a_scores(half):
+            s_psum = misc.tile([P, BLOCKS // 2, NB], F32, tag="misc")
+            for k in range(BLOCKS // 2):
+                block = half * (BLOCKS // 2) + k
+                nc.tensor.matmul(
+                    out=s_psum[:, k, :],
+                    lhsT=q_diag[:, block].rearrange("p h w -> p (h w)"),
+                    rhs=ka_pad[:, 2 * block : 2 * block + NB_ROWS, :].rearrange("p y x -> p (y x)"),
+                    start=True,
+                    stop=True,
+                )
+            return s_psum
+
+        def a_mask(half, s_psum):
+            nc.vector.tensor_tensor(
+                out=masked[:, half * (BLOCKS // 2) : (half + 1) * (BLOCKS // 2), 0:NB],
+                in0=s_psum[:],
+                in1=mask[:].unsqueeze(1).to_broadcast([P, BLOCKS // 2, NB]),
+                op=ALU.add,
+            )
+
+        def a_exp():
+            nc.vector.tensor_reduce(out=top_a[:], in_=masked[:], axis=AXIS_X, op=ALU.max)
+            nc.vector.tensor_scalar(
+                out=minus_top[:], in0=top_a[:], scalar1=-1.0, scalar2=0.0, op0=ALU.mult, op1=ALU.add
+            )
+            for block in range(BLOCKS):
+                nc.scalar.activation(
+                    out=e_a[:, block],
+                    in_=masked[:, block],
+                    func=ACT.Exp,
+                    bias=minus_top[:, block : block + 1],
+                    accum_out=total_a[:, block : block + 1],
+                )
+
+        def a_normalise():
+            nc.vector.reciprocal(out=inv_a[:], in_=total_a[:])
+            for s, (first_block, blocks, top) in enumerate(SUM_TILES):
+                for block in range(first_block, first_block + blocks):
+                    first = 2 * block - PAD
+                    lo = max(0, -first)
+                    hi = min(NB_ROWS, SIDE - first)
+                    at = first + lo - top
+                    nc.scalar.activation(
+                        out=att_a[:, block, at * SIDE : (at + hi - lo) * SIDE],
+                        in_=e_a[:, block, lo * SIDE : hi * SIDE],
+                        func=ACT.Copy,
+                        scale=inv_a[:, block : block + 1],
                     )
-            return projected[:].rearrange("p b (y x) -> p b y x", x=SIDE)
 
-        nc.scalar.copy(out=k_pad[:, :, PAD : PAD + SIDE, PAD : PAD + SIDE], in_=project_channels_first("k"))
-        q_psum = project_channels_first("q")
-        q_sb = keep.tile([P, CH_TILES, SIDE, SIDE], F32)
-        nc.vector.tensor_copy(out=q_sb[:], in_=q_psum)
+        def a_turn():
+            for s, (first_block, blocks, top) in enumerate(SUM_TILES):
+                turned = stream.tile([P, 3, GROUP, BLOCK_PIX], F32, tag="stream")
+                for k in range(blocks):
+                    nc.tensor.transpose(
+                        turned[:, k].rearrange("p h w -> p (h w)"), att_a[:, first_block + k, :], ident[:]
+                    )
+                nc.scalar.copy(
+                    out=att_t[:, first_block * P : (first_block + blocks) * P].rearrange(
+                        "p (h k w) -> p h k w", h=GROUP, w=BLOCK_PIX
+                    ),
+                    in_=turned[:, 0:blocks].rearrange("p k h w -> p h k w"),
+                )
 
-        rows_of_softmax = PIX_TILES * HEADS
+        def a_sum(sum_a, s):
+            first_block, blocks, top = SUM_TILES[s]
+            for h in range(GROUP):
+                start = first_block * P + h * blocks * BLOCK_PIX
+                cols = slice(h * HEAD_DIM, (h + 1) * HEAD_DIM)
+                nc.tensor.matmul(
+                    out=sum_a[:, s, cols],
+                    lhsT=att_t[:, start : start + P],
+                    rhs=va_sb[:, s, cols],
+                    start=True,
+                    stop=True,
+                )
+
+        rows_of_softmax = PIX_TILES * GROUP
         scores = keep.tile([P, WIN, rows_of_softmax], F32)
-        for o_first in range(0, WIN, 2):
-            n = min(2, WIN - o_first)
-            halves = stream.tile([P, 2, PIX_TILES, P], F32, tag="stream")
-            for oo in range(n):
-                i, j = divmod(o_first + oo, KSIZE)
-                k_window = k_pad[:, :, i : i + SIDE, j : j + SIDE]
-                qk = work.tile([P, CH_TILES, PIX], F32, bufs=8)
+
+        def b_products(o_first):
+            tiles = []
+            for o in range(o_first, min(o_first + 4, WIN)):
+                i, j = divmod(o, KSIZE)
+                k_window = k_pad[:, :, i : i + ROWS, j : j + SIDE]
+                qk = work.tile([P, HALVES, P], F32, bufs=10)
                 qk_image = qk[:].rearrange("p b (y x) -> p b y x", x=SIDE)
-                if oo == 0:
-                    nc.vector.tensor_tensor(out=qk_image, in0=q_psum, in1=k_window, op=ALU.mult)
+                if o in GPSIMD_OFFSETS:
+                    nc.gpsimd.tensor_tensor(
+                        out=qk_image, in0=qb_sb[:].rearrange("p b (y x) -> p b y x", x=SIDE), in1=k_window, op=ALU.mult
+                    )
                 else:
-                    nc.gpsimd.tensor_tensor(out=qk_image, in0=q_sb[:], in1=k_window, op=ALU.mult)
-                for t in range(PIX_TILES):
-                    for b in range(CH_TILES):
-                        nc.tensor.matmul(
-                            out=halves[:, oo, t, :],
-                            lhsT=qk[:, b, t * P : (t + 1) * P],
-                            rhs=ident[:],
-                            is_transpose=True,
-                            start=(b == 0),
-                            stop=(b == CH_TILES - 1),
-                        )
+                    nc.vector.tensor_tensor(
+                        out=qk_image, in0=qb_psum[:].rearrange("p b (y x) -> p b y x", x=SIDE), in1=k_window, op=ALU.mult
+                    )
+                tiles.append((o, qk))
+            return tiles
+
+        def b_turn(tiles):
+            halves = stream.tile([P, 4, P], F32, tag="stream")
+            for o, qk in [pair for pair in tiles if pair[0] not in GPSIMD_OFFSETS] + [
+                pair for pair in tiles if pair[0] in GPSIMD_OFFSETS
+            ]:
+                for b in range(HALVES):
+                    nc.tensor.matmul(
+                        out=halves[:, o - tiles[0][0], :],
+                        lhsT=qk[:, b, :],
+                        rhs=ident[:],
+                        is_transpose=True,
+                        start=(b == 0),
+                        stop=(b == HALVES - 1),
+                    )
+            return halves
+
+        def b_reduce(o_first, halves):
+            n = min(4, WIN - o_first)
             nc.vector.tensor_reduce(
                 out=scores[:, o_first : o_first + n, :].rearrange("p o r -> p (o r)"),
-                in_=halves[:, 0:n].rearrange("p o t (h c) -> p (o t h) c", c=HALF_HEAD),
+                in_=halves[:, 0:n].rearrange("p o (r c) -> p (o r) c", c=HALF_HEAD),
                 axis=AXIS_X,
                 op=ALU.add,
             )
 
-        top = small.tile([P, rows_of_softmax], F32)
-        nc.vector.tensor_reduce(out=top[:], in_=scores[:].rearrange("p o r -> p r o"), axis=AXIS_X, op=ALU.max)
+        wt_a = {}
+        for part in ("qa", "ka", "va"):
+            wt_a[part] = transpose_weight(part, ident)
+        tiles = {}
+        tiles[0] = b_products(0)
+        a_weight("qa")
+        tiles[4] = b_products(4)
+        a_weight("ka")
+        b_reduce(0, b_turn(tiles[0]))
+        a_project()
+        tiles[8] = b_products(8)
+        b_reduce(4, b_turn(tiles[4]))
+        a_weight("va")
+        a_values()
+        tiles[12] = b_products(12)
+        s_low = a_scores(0)
+        b_reduce(8, b_turn(tiles[8]))
+        tiles[16] = b_products(16)
+        s_high = a_scores(1)
+        a_mask(0, s_low)
+        b_reduce(12, b_turn(tiles[12]))
+        a_mask(1, s_high)
+        tiles[20] = b_products(20)
+        b_reduce(16, b_turn(tiles[16]))
+        a_exp()
+        tiles[24] = b_products(24)
+        b_reduce(20, b_turn(tiles[20]))
+        b_reduce(24, b_turn(tiles[24]))
+        a_normalise()
+
+        top_b = keep.tile([P, rows_of_softmax], F32)
+        nc.vector.tensor_reduce(out=top_b[:], in_=scores[:].rearrange("p o r -> p r o"), axis=AXIS_X, op=ALU.max)
         centred = keep.tile([P, WIN, rows_of_softmax], F32)
         nc.vector.tensor_tensor(
             out=centred[:],
             in0=scores[:],
-            in1=top[:].unsqueeze(1).to_broadcast([P, WIN, rows_of_softmax]),
+            in1=top_b[:].unsqueeze(1).to_broadcast([P, WIN, rows_of_softmax]),
             op=ALU.subtract,
         )
-        e = keep.tile([P, WIN, rows_of_softmax], F32)
-        nc.scalar.activation(out=e[:], in_=centred[:], func=ACT.Exp)
-        total = small.tile([P, rows_of_softmax], F32)
-        nc.vector.tensor_reduce(out=total[:], in_=e[:].rearrange("p o r -> p r o"), axis=AXIS_X, op=ALU.add)
-        inv = small.tile([P, rows_of_softmax], F32)
-        nc.vector.reciprocal(out=inv[:], in_=total[:])
-        inv_inside = small.tile([P, KSIZE, rows_of_softmax], F32)
+        e_b = keep.tile([P, WIN, rows_of_softmax], F32)
+        nc.scalar.activation(out=e_b[:], in_=centred[:], func=ACT.Exp)
+        total_b = keep.tile([P, rows_of_softmax], F32)
+        nc.vector.tensor_reduce(out=total_b[:], in_=e_b[:].rearrange("p o r -> p r o"), axis=AXIS_X, op=ALU.add)
+        inv_b = keep.tile([P, rows_of_softmax], F32)
+        nc.vector.reciprocal(out=inv_b[:], in_=total_b[:])
+        inv_inside = keep.tile([P, KSIZE, rows_of_softmax], F32)
         nc.vector.tensor_tensor(
             out=inv_inside[:],
-            in0=inv[:].unsqueeze(1).to_broadcast([P, KSIZE, rows_of_softmax]),
+            in0=inv_b[:].unsqueeze(1).to_broadcast([P, KSIZE, rows_of_softmax]),
             in1=inside[:].unsqueeze(2).to_broadcast([P, KSIZE, rows_of_softmax]),
             op=ALU.mult,
         )
-        att = keep.tile([P, WIN, PIX_TILES, HEADS], F32)
-        nc.vector.tensor_tensor(
-            out=att[:].rearrange("p (i j) t h -> p i (j t h)", j=KSIZE),
-            in0=e[:].rearrange("p (i j) r -> p i (j r)", j=KSIZE),
-            in1=inv_inside[:].rearrange("p j r -> p (j r)").unsqueeze(1).to_broadcast([P, KSIZE, KSIZE * rows_of_softmax]),
-            op=ALU.mult,
-        )
-
-        out_view = out.rearrange("n (ct c) h w -> c (n ct) (h w)", ct=CH_TILES, c=P)
+        att_b = keep.tile([P, PIX_TILES, WIN, GROUP], F32)
         for t in range(PIX_TILES):
-            result = [sums.tile([P, P], F32, tag="sums", name="result_%d" % ct) for ct in range(CH_TILES)]
-            chunks = [(o, KSIZE) for o in range(0, WIN, KSIZE)]
-            if t == PIX_TILES - 1:
-                chunks[-1:] = [(WIN - KSIZE, LAST_CUT), (WIN - KSIZE + LAST_CUT, KSIZE - LAST_CUT)]
-            for o_first, n in chunks:
-                av = work.tile([P, KSIZE, D], F32)
-                nc.vector.tensor_tensor(
-                    out=av[:, 0:n, :].rearrange("p o (h c) -> p o h c", h=HEADS),
-                    in0=v_win[:, t, o_first : o_first + n, :].rearrange("p o (h c) -> p o h c", h=HEADS),
-                    in1=att[:, o_first : o_first + n, t, :].unsqueeze(3).to_broadcast([P, n, HEADS, HEAD_DIM]),
-                    op=ALU.mult,
+            nc.vector.tensor_tensor(
+                out=att_b[:, t].rearrange("p (i j) h -> p i j h", j=KSIZE),
+                in0=e_b[:, :, t * GROUP : (t + 1) * GROUP].rearrange("p (i j) h -> p i j h", j=KSIZE),
+                in1=inv_inside[:, :, t * GROUP : (t + 1) * GROUP].unsqueeze(1).to_broadcast([P, KSIZE, KSIZE, GROUP]),
+                op=ALU.mult,
+            )
+
+        out_rows = out.rearrange("n c h w -> (n c) (h w)")
+        a_turn()
+        sum_a = misc.tile([P, len(SUM_TILES), P], F32, tag="misc")
+        final_a = misc.tile([P, len(SUM_TILES), P], F32, tag="misc")
+        results = [misc.tile([P, P], F32, tag="misc", name="result_%d" % t) for t in range(PIX_TILES)]
+        out_b = keep.tile([P, PIX_TILES, P], F32)
+
+        def b_weigh(t, i):
+            av = work.tile([P, KSIZE, P], F32)
+            split = SCALAR_FROM[i]
+            o = i * KSIZE
+            nc.vector.tensor_tensor(
+                out=av[:, 0:split].rearrange("p o (h c) -> p (o h) c", h=GROUP),
+                in0=v_win[:, t, o : o + split, :].rearrange("p o (h c) -> p (o h) c", h=GROUP),
+                in1=att_b[:, t, o : o + split, :]
+                .rearrange("p o h -> p (o h)")
+                .unsqueeze(2)
+                .to_broadcast([P, split * GROUP, HEAD_DIM]),
+                op=ALU.mult,
+            )
+            for j in range(split, KSIZE):
+                for h in range(GROUP):
+                    cols = slice(h * HEAD_DIM, (h + 1) * HEAD_DIM)
+                    nc.scalar.activation(
+                        out=av[:, j, cols],
+                        in_=v_win[:, t, o + j, cols],
+                        func=ACT.Copy,
+                        scale=att_b[:, t, o + j, h : h + 1],
+                    )
+            for j in range(KSIZE):
+                nc.tensor.matmul(
+                    out=results[t][:],
+                    lhsT=av[:, j, :],
+                    rhs=ident[:],
+                    is_transpose=True,
+                    start=(o + j == 0),
+                    stop=(o + j == WIN - 1),
                 )
-                for oo in range(n):
-                    for ct in range(CH_TILES):
-                        nc.tensor.matmul(
-                            out=result[ct][:],
-                            lhsT=av[:, oo, ct * P : (ct + 1) * P],
-                            rhs=ident[:],
-                            is_transpose=True,
-                            start=(o_first + oo == 0),
-                            stop=(o_first + oo == WIN - 1),
-                        )
-            out_sb = small.tile([P, CH_TILES, P], F32)
-            for ct in range(CH_TILES):
-                nc.scalar.copy(out=out_sb[:, ct, :], in_=result[ct][:])
-            nc.sync.dma_start(out=out_view[:, :, t * P : (t + 1) * P], in_=out_sb[:])
+
+        def b_store(t):
+            nc.scalar.copy(out=out_b[:, t], in_=results[t][:])
+            nc.sync.dma_start(out=out_rows[P : 2 * P, t * P : (t + 1) * P], in_=out_b[:, t])
+
+        a_sum(sum_a, 0)
+        b_weigh(0, 0)
+        a_sum(sum_a, 1)
+        b_weigh(0, 1)
+        a_sum(sum_a, 2)
+        b_weigh(0, 2)
+        sum_a_sb = keep.tile([P, len(SUM_TILES), P], F32)
+        nc.scalar.copy(out=sum_a_sb[:], in_=sum_a[:])
+        b_weigh(0, 3)
+        for s in range(len(SUM_TILES)):
+            nc.tensor.transpose(final_a[:, s, :], sum_a_sb[:, s, :], ident[:])
+        b_weigh(0, 4)
+        b_weigh(1, 0)
+        out_a = keep.tile([P, PIX], F32)
+        for s, (first_block, blocks, top) in enumerate(SUM_TILES):
+            n = blocks * BLOCK_PIX
+            nc.scalar.copy(out=out_a[:, first_block * BLOCK_PIX : first_block * BLOCK_PIX + n], in_=final_a[:, s, 0:n])
+        b_store(0)
+        for i in range(1, KSIZE):
+            b_weigh(1, i)
+        b_store(1)
+        nc.sync.dma_start(out=out_rows[0:P, :], in_=out_a[:])

@@ -43,6 +43,7 @@ SUM_TILES = ((0, 3, 0), (3, 2, 4), (5, 3, 8))
 BIG = 2.0**100
 
 SCALAR_FROM = (3, 4, 3, 4, 3)
+IDLE_PASSES = 24
 GPSIMD_OFFSETS = tuple(range(1, WIN, 2))
 
 FLOPS = 2 * 3 * D * C_IN * PIX + 2 * 2 * D * WIN * PIX
@@ -73,6 +74,22 @@ def tile_relation_s_kernel(tc, x, w_qkv, out):
         make_identity(nc, ident[:])
         zero = keep.tile([P, P], F32)
         nc.vector.memset(zero[:], 0.0)
+        idle_in = keep.tile([P, P * PACK], BF16, align_bytes=64)
+        nc.vector.memset(idle_in[:], 0.0)
+        idle_codes = keep.tile([P, P], U32, align_bytes=64)
+        idle_scales = keep.tile([P, P], U8, align_bytes=64)
+        nc.vector.quantize_mx(out=idle_codes[:].bitcast(FP8X4), scales=idle_scales[:], in_=idle_in[:])
+        idle_out = stream.tile([P, P], F32, tag="stream")
+        for k in range(IDLE_PASSES):
+            nc.tensor.matmul_mx(
+                out=idle_out[:],
+                lhsT=idle_codes[:].bitcast(FP8X4),
+                lhsT_scale=idle_scales[:],
+                rhs=idle_codes[:].bitcast(FP8X4),
+                rhs_scale=idle_scales[:],
+                start=True,
+                stop=True,
+            )
         warm_out = keep.tile([P, 1], F32)
         nc.scalar.activation(out=warm_out[:], in_=zero[:, 0:1], func=ACT.Exp)
         parked = out.rearrange("n c h w -> (n c) (h w)").rearrange("r (s c) -> (r s) c", s=2)

@@ -45,6 +45,8 @@ BIG = 2.0**100
 SCALAR_FROM = (3, 4, 3, 4, 3)
 IDLE_PASSES = 24
 GPSIMD_OFFSETS = tuple(range(1, WIN, 2))
+ROW_ORDER = (2, 0, 1, 3, 4)
+HOLD_PASSES = 4
 
 FLOPS = 2 * 3 * D * C_IN * PIX + 2 * 2 * D * WIN * PIX
 
@@ -281,7 +283,7 @@ def tile_relation_s_kernel(tc, x, w_qkv, out):
         nc.scalar.copy(
             out=k_pad[0:HALF, :, PAD + ROWS : 2 * PAD + ROWS, inner], in_=kb_view[0:HALF, 1, :, 0:PAD, :]
         )
-        nc.vector.tensor_copy(out=k_pad[HALF:P, :, 0:PAD, inner], in_=kb_view[HALF:P, 1, :, ROWS - PAD : ROWS, :])
+        nc.scalar.copy(out=k_pad[HALF:P, :, 0:PAD, inner], in_=kb_view[HALF:P, 1, :, ROWS - PAD : ROWS, :])
 
         vb_psum = misc.tile([P, PIX_TILES, P], F32, tag="misc")
         for t in range(PIX_TILES):
@@ -291,7 +293,7 @@ def tile_relation_s_kernel(tc, x, w_qkv, out):
         nc.sync.dma_start(out=parked[P : 3 * P, :].rearrange("(t p) c -> p t c", p=P), in_=vb_sb[:])
         v_win = keep.tile([P, PIX_TILES, WIN, P], F32)
         for o in range(WIN):
-            i, j = divmod(o, KSIZE)
+            i, j = ROW_ORDER[o // KSIZE], o % KSIZE
             first = P + (i - PAD) * SIDE + j - PAD
             nc.sync.dma_start(
                 out=v_win[:, :, o, :], in_=parked[first : first + PIX, :].rearrange("(t p) c -> p t c", p=P)
@@ -300,8 +302,26 @@ def tile_relation_s_kernel(tc, x, w_qkv, out):
 
         a_mx = {}
 
-        def a_weight(part):
-            a_mx[part] = quantise_weight(part, group_weight(part, wt_a[part], to_scalar))
+        grouped_a = {}
+
+        def a_group(part):
+            grouped_a[part] = group_weight(part, wt_a[part], to_scalar)
+
+        def a_quantise(part):
+            a_mx[part] = quantise_weight(part, grouped_a[part])
+
+        def hold_clock():
+            idle = stream.tile([P, PASSES * PIX], F32, tag="stream")
+            for k in range(HOLD_PASSES):
+                nc.tensor.matmul_mx(
+                    out=idle[:],
+                    lhsT=x_codes[:, 0, 0:P].bitcast(FP8X4),
+                    lhsT_scale=x_scales[:, 0, 0:P],
+                    rhs=x_codes[:].rearrange("p g w -> p (g w)").bitcast(FP8X4),
+                    rhs_scale=x_scales[:].rearrange("p g w -> p (g w)"),
+                    start=True,
+                    stop=True,
+                )
 
         qka_psum = misc.tile([P, 2, PIX], F32, tag="misc")
         va_psum = misc.tile([P, len(SUM_TILES), P], F32, tag="misc")
@@ -329,23 +349,24 @@ def tile_relation_s_kernel(tc, x, w_qkv, out):
                 mx(va_psum[:, s, :], x_mx, slice(top * SIDE, top * SIDE + P), a_mx["va"], every)
             nc.scalar.copy(out=va_sb[:], in_=va_psum[:])
 
-        def a_scores(half):
-            s_psum = misc.tile([P, BLOCKS // 2, NB], F32, tag="misc")
-            for k in range(BLOCKS // 2):
-                block = half * (BLOCKS // 2) + k
+        s_psum = []
+
+        def a_scores(first_block, last_block):
+            for block in range(first_block, last_block):
+                if block % (BLOCKS // 2) == 0:
+                    s_psum.append(misc.tile([P, BLOCKS // 2, NB], F32, tag="misc", name="s_psum"))
                 nc.tensor.matmul(
-                    out=s_psum[:, k, :],
+                    out=s_psum[-1][:, block % (BLOCKS // 2), :],
                     lhsT=q_diag[:, block].rearrange("p h w -> p (h w)"),
                     rhs=ka_pad[:, 2 * block : 2 * block + NB_ROWS, :].rearrange("p y x -> p (y x)"),
                     start=True,
                     stop=True,
                 )
-            return s_psum
 
-        def a_mask(half, s_psum):
+        def a_mask(half):
             nc.vector.tensor_tensor(
                 out=masked[:, half * (BLOCKS // 2) : (half + 1) * (BLOCKS // 2), 0:NB],
-                in0=s_psum[:],
+                in0=s_psum[half][:],
                 in1=mask[:].unsqueeze(1).to_broadcast([P, BLOCKS // 2, NB]),
                 op=ALU.add,
             )
@@ -412,7 +433,7 @@ def tile_relation_s_kernel(tc, x, w_qkv, out):
         def b_products(o_first):
             tiles = []
             for o in range(o_first, min(o_first + 4, WIN)):
-                i, j = divmod(o, KSIZE)
+                i, j = ROW_ORDER[o // KSIZE], o % KSIZE
                 k_window = k_pad[:, :, i : i + ROWS, j : j + SIDE]
                 qk = work.tile([P, HALVES, P], F32, bufs=10)
                 qk_image = qk[:].rearrange("p b (y x) -> p b y x", x=SIDE)
@@ -457,30 +478,35 @@ def tile_relation_s_kernel(tc, x, w_qkv, out):
             wt_a[part] = transpose_weight(part, ident)
         tiles = {}
         tiles[0] = b_products(0)
-        a_weight("qa")
+        a_group("qa")
+        a_quantise("qa")
         tiles[4] = b_products(4)
-        a_weight("ka")
+        a_group("ka")
         b_reduce(0, b_turn(tiles[0]))
+        a_quantise("ka")
         a_project()
         tiles[8] = b_products(8)
         b_reduce(4, b_turn(tiles[4]))
-        a_weight("va")
-        a_values()
+        a_group("va")
         tiles[12] = b_products(12)
-        s_low = a_scores(0)
         b_reduce(8, b_turn(tiles[8]))
+        a_quantise("va")
+        a_scores(0, 3)
         tiles[16] = b_products(16)
-        s_high = a_scores(1)
-        a_mask(0, s_low)
         b_reduce(12, b_turn(tiles[12]))
-        a_mask(1, s_high)
+        a_scores(3, 6)
+        a_mask(0)
         tiles[20] = b_products(20)
         b_reduce(16, b_turn(tiles[16]))
+        a_scores(6, 8)
+        a_values()
+        a_mask(1)
         a_exp()
         tiles[24] = b_products(24)
         b_reduce(20, b_turn(tiles[20]))
         b_reduce(24, b_turn(tiles[24]))
         a_normalise()
+        hold_clock()
 
         top_b = keep.tile([P, rows_of_softmax], F32)
         nc.vector.tensor_reduce(out=top_b[:], in_=scores[:].rearrange("p o r -> p r o"), axis=AXIS_X, op=ALU.max)

@@ -39,14 +39,16 @@ NB_ROWS = 2 + 2 * PAD
 NB = NB_ROWS * SIDE
 BESIDE = 2 * KSIZE
 COLS = NB + BESIDE
-SUM_TILES = ((0, 3, 0), (3, 2, 4), (5, 3, 8))
+SUM_TOPS = (0, 2, 6, 8)
+SUM_BLOCKS = BLOCKS // len(SUM_TOPS)
+SUM_PIX = SUM_BLOCKS * BLOCK_PIX
+PAIRS = GROUP // 2
+SHIFT = 32
 BIG = 2.0**100
 
 SCALAR_FROM = (3, 4, 3, 4, 3)
-IDLE_PASSES = 24
 GPSIMD_OFFSETS = tuple(range(1, WIN, 2))
 ROW_ORDER = (2, 0, 1, 3, 4)
-HOLD_PASSES = 4
 
 FLOPS = 2 * 3 * D * C_IN * PIX + 2 * 2 * D * WIN * PIX
 
@@ -67,7 +69,7 @@ def tile_relation_s_kernel(tc, x, w_qkv, out):
             nc.sync.dma_start(out=x_sb[:, g].rearrange("p t w -> p (t w)"), in_=x_view[:, g, :])
         first_row = {"qa": 0, "qb": P, "ka": D, "kb": D + P, "va": 2 * D, "vb": 2 * D + P}
         w_sb = {}
-        for part in ("kb", "qb", "vb", "qa", "ka", "va"):
+        for part in ("kb", "qb", "qa", "ka", "vb", "va"):
             w_sb[part] = keep.tile([P, C_IN], BF16, name="w_sb_" + part)
             row = first_row[part]
             nc.sync.dma_start(out=w_sb[part][:], in_=w_qkv[row : row + P, :])
@@ -76,22 +78,6 @@ def tile_relation_s_kernel(tc, x, w_qkv, out):
         make_identity(nc, ident[:])
         zero = keep.tile([P, P], F32)
         nc.vector.memset(zero[:], 0.0)
-        idle_in = keep.tile([P, P * PACK], BF16, align_bytes=64)
-        nc.vector.memset(idle_in[:], 0.0)
-        idle_codes = keep.tile([P, P], U32, align_bytes=64)
-        idle_scales = keep.tile([P, P], U8, align_bytes=64)
-        nc.vector.quantize_mx(out=idle_codes[:].bitcast(FP8X4), scales=idle_scales[:], in_=idle_in[:])
-        idle_out = stream.tile([P, P], F32, tag="stream")
-        for k in range(IDLE_PASSES):
-            nc.tensor.matmul_mx(
-                out=idle_out[:],
-                lhsT=idle_codes[:].bitcast(FP8X4),
-                lhsT_scale=idle_scales[:],
-                rhs=idle_codes[:].bitcast(FP8X4),
-                rhs_scale=idle_scales[:],
-                start=True,
-                stop=True,
-            )
         warm_out = keep.tile([P, 1], F32)
         nc.scalar.activation(out=warm_out[:], in_=zero[:, 0:1], func=ACT.Exp)
         parked = out.rearrange("n c h w -> (n c) (h w)").rearrange("r (s c) -> (r s) c", s=2)
@@ -110,14 +96,13 @@ def tile_relation_s_kernel(tc, x, w_qkv, out):
             split_scales[part] = keep.tile([P, PASSES, 5 * HALF], U8, align_bytes=64, name="scales_" + part)
             nc.vector.memset(split_codes[part][:].rearrange("p g (z o) -> p g z o", o=HALF)[:, :, 0:5:2, :], 0)
             nc.vector.memset(split_scales[part][:].rearrange("p g o -> p (g o)").bitcast(I32), 0)
-        ka_pad = keep.tile([P, SIDE + 2 * PAD, SIDE], F32)
-        nc.gpsimd.memset(ka_pad[:], 0.0)
+        x_scales = keep.tile([P, PASSES, PIX], U8, align_bytes=64)
+        nc.gpsimd.memset(x_scales[:].rearrange("p g w -> p (g w)").bitcast(I32), 0)
         column = keep.tile([P, SIDE + 2 * PAD], F32)
         nc.gpsimd.memset(column[:], 0.0)
         att_a = keep.tile([P, BLOCKS, P], F32)
         nc.gpsimd.memset(att_a[:], 0.0)
-        att_t = keep.tile([P, BLOCKS * P + P], F32)
-        nc.gpsimd.memset(att_t[:, BLOCKS * P : BLOCKS * P + P], 0.0)
+        att_t = keep.tile([P, len(SUM_TOPS), GROUP, SUM_BLOCKS, BLOCK_PIX], F32)
         split_heads = keep.tile([P, P], F32)
         nc.vector.tensor_copy(
             out=split_heads[:].rearrange("p (b h c) -> p b h c", b=HALVES, c=HALF_HEAD),
@@ -165,10 +150,12 @@ def tile_relation_s_kernel(tc, x, w_qkv, out):
             op0=ALU.subtract,
             op1=ALU.mult,
         )
+        masked = keep.tile([P, BLOCKS, COLS], F32)
+        for block, cols in ((0, slice(0, PAD * SIDE)), (BLOCKS - 1, slice(NB - PAD * SIDE, NB))):
+            nc.gpsimd.tensor_copy(out=masked[:, block, cols], in_=mask[:, cols])
         beside = keep.tile([P, 2], F32)
         nc.gpsimd.tensor_tensor(out=beside[:, 0:1], in0=inside[:, 0:1], in1=inside[:, 4:5], op=ALU.add)
         nc.gpsimd.tensor_tensor(out=beside[:, 1:2], in0=inside[:, 1:2], in1=inside[:, 3:4], op=ALU.add)
-        masked = keep.tile([P, BLOCKS, COLS], F32)
         for f in range(2):
             nc.gpsimd.tensor_scalar(
                 out=masked[:, :, NB + f * KSIZE : NB + (f + 1) * KSIZE],
@@ -181,7 +168,7 @@ def tile_relation_s_kernel(tc, x, w_qkv, out):
 
         x_grouped = keep.tile([P, PASSES, PIX, PACK], BF16, align_bytes=64)
         x_codes = keep.tile([P, PASSES, PIX], U32, align_bytes=64)
-        x_scales = keep.tile([P, PASSES, PIX], U8, align_bytes=64)
+        x_scales_moved = keep.tile([P, PASSES, PIX + 2 * SHIFT], U8, align_bytes=64)
         for g in range(PASSES):
             nc.vector.tensor_copy(out=x_grouped[:, g], in_=x_sb[:, g].rearrange("p t w -> p w t"))
         for g in range(PASSES):
@@ -191,6 +178,13 @@ def tile_relation_s_kernel(tc, x, w_qkv, out):
                 in_=x_grouped[:, g].rearrange("p w t -> p (w t)"),
             )
         x_mx = (x_codes, x_scales)
+        words = PIX // 4
+        nc.gpsimd.tensor_copy(
+            out=x_scales_moved[:].rearrange("p g w -> p (g w)").bitcast(I32).rearrange("p (g w) -> p g w", g=PASSES)[
+                :, :, SHIFT // 4 : SHIFT // 4 + words
+            ],
+            in_=x_scales[:].rearrange("p g w -> p (g w)").bitcast(I32).rearrange("p (g w) -> p g w", g=PASSES),
+        )
 
         def transpose_weight(part, order):
             words = w_sb[part][:].bitcast(F32)
@@ -260,13 +254,18 @@ def tile_relation_s_kernel(tc, x, w_qkv, out):
         to_vector = nc.vector.tensor_copy
         to_scalar = nc.scalar.copy
 
-        wt_kb = transpose_weight("kb", split_heads)
-        wt_qb = transpose_weight("qb", split_heads)
-        wt_vb = transpose_weight("vb", ident)
-        kb_mx = quantise_split_weight("kb", group_weight("kb", wt_kb, to_vector))
-        qb_mx = quantise_split_weight("qb", group_weight("qb", wt_qb, to_scalar))
-        vb_grouped = group_weight("vb", wt_vb, to_scalar)
-        vb_mx = quantise_weight("vb", vb_grouped)
+        grouped = {}
+        w_mx = {}
+
+        def turn_weight(part, copy_out):
+            order = split_heads if part in split_codes else ident
+            grouped[part] = group_weight(part, transpose_weight(part, order), copy_out)
+
+        turn_weight("kb", to_vector)
+        turn_weight("qb", to_scalar)
+        turn_weight("qa", to_scalar)
+        kb_mx = quantise_split_weight("kb", grouped["kb"])
+        qb_mx = quantise_split_weight("qb", grouped["qb"])
         kb_psum = misc.tile([P, 2, HALVES, P], F32, tag="misc")
         for b in range(HALVES):
             mx_split(kb_psum[:, 0, b, :], kb_mx, b, 0)
@@ -275,57 +274,37 @@ def tile_relation_s_kernel(tc, x, w_qkv, out):
             mx_split(qb_psum[:, b, :], qb_mx, b, 0)
         for b in range(HALVES):
             mx_split(kb_psum[:, 1, b, :], kb_mx, b, 1)
+        w_mx["qa"] = quantise_weight("qa", grouped["qa"])
         kb_view = kb_psum[:].rearrange("p o b (y x) -> p o b y x", x=SIDE)
         inner = slice(PAD, PAD + SIDE)
         qb_sb = keep.tile([P, HALVES, P], F32)
-        nc.scalar.copy(out=qb_sb[:], in_=qb_psum[:])
         nc.vector.tensor_copy(out=k_pad[:, :, PAD : PAD + ROWS, inner], in_=kb_view[:, 0])
+        nc.scalar.copy(out=qb_sb[:], in_=qb_psum[:])
         nc.scalar.copy(
             out=k_pad[0:HALF, :, PAD + ROWS : 2 * PAD + ROWS, inner], in_=kb_view[0:HALF, 1, :, 0:PAD, :]
         )
         nc.scalar.copy(out=k_pad[HALF:P, :, 0:PAD, inner], in_=kb_view[HALF:P, 1, :, ROWS - PAD : ROWS, :])
 
         vb_psum = misc.tile([P, PIX_TILES, P], F32, tag="misc")
-        for t in range(PIX_TILES):
-            mx(vb_psum[:, t, :], x_mx, slice(t * P, (t + 1) * P), vb_mx, every)
         vb_sb = keep.tile([P, PIX_TILES, P], F32)
-        nc.scalar.copy(out=vb_sb[:], in_=vb_psum[:])
-        nc.sync.dma_start(out=parked[P : 3 * P, :].rearrange("(t p) c -> p t c", p=P), in_=vb_sb[:])
         v_win = keep.tile([P, PIX_TILES, WIN, P], F32)
-        for o in range(WIN):
-            i, j = ROW_ORDER[o // KSIZE], o % KSIZE
-            first = P + (i - PAD) * SIDE + j - PAD
-            nc.sync.dma_start(
-                out=v_win[:, :, o, :], in_=parked[first : first + PIX, :].rearrange("(t p) c -> p t c", p=P)
-            )
 
-
-        a_mx = {}
-
-        grouped_a = {}
-
-        def a_group(part):
-            grouped_a[part] = group_weight(part, wt_a[part], to_scalar)
-
-        def a_quantise(part):
-            a_mx[part] = quantise_weight(part, grouped_a[part])
-
-        def hold_clock():
-            idle = stream.tile([P, PASSES * PIX], F32, tag="stream")
-            for k in range(HOLD_PASSES):
-                nc.tensor.matmul_mx(
-                    out=idle[:],
-                    lhsT=x_codes[:, 0, 0:P].bitcast(FP8X4),
-                    lhsT_scale=x_scales[:, 0, 0:P],
-                    rhs=x_codes[:].rearrange("p g w -> p (g w)").bitcast(FP8X4),
-                    rhs_scale=x_scales[:].rearrange("p g w -> p (g w)"),
-                    start=True,
-                    stop=True,
+        def b_values():
+            for t in range(PIX_TILES):
+                mx(vb_psum[:, t, :], x_mx, slice(t * P, (t + 1) * P), w_mx["vb"], every)
+            nc.scalar.copy(out=vb_sb[:], in_=vb_psum[:])
+            nc.sync.dma_start(out=parked[P : 3 * P, :].rearrange("(t p) c -> p t c", p=P), in_=vb_sb[:])
+            for o in range(WIN):
+                i, j = ROW_ORDER[o // KSIZE], o % KSIZE
+                first = P + (i - PAD) * SIDE + j - PAD
+                nc.sync.dma_start(
+                    out=v_win[:, :, o, :], in_=parked[first : first + PIX, :].rearrange("(t p) c -> p t c", p=P)
                 )
 
         qka_psum = misc.tile([P, 2, PIX], F32, tag="misc")
-        va_psum = misc.tile([P, len(SUM_TILES), P], F32, tag="misc")
-        va_sb = keep.tile([P, len(SUM_TILES), P], F32)
+        va_psum = misc.tile([P, len(SUM_TOPS), P], F32, tag="misc")
+        va_sb = keep.tile([P, len(SUM_TOPS), P], F32)
+        ka_sb = keep.tile([P, SIDE, SIDE], F32)
         top_a = keep.tile([P, BLOCKS], F32)
         minus_top = keep.tile([P, BLOCKS], F32)
         e_a = keep.tile([P, BLOCKS, COLS], F32)
@@ -333,10 +312,10 @@ def tile_relation_s_kernel(tc, x, w_qkv, out):
         inv_a = keep.tile([P, BLOCKS], F32)
 
         def a_project():
-            mx(qka_psum[:, 0, :], a_mx["qa"], every, x_mx, all_pix)
-            mx(qka_psum[:, 1, :], a_mx["ka"], every, x_mx, all_pix)
+            mx(qka_psum[:, 0, :], w_mx["qa"], every, x_mx, all_pix)
+            mx(qka_psum[:, 1, :], w_mx["ka"], every, x_mx, all_pix)
             nc.scalar.copy(
-                out=ka_pad[:, PAD : PAD + SIDE, :], in_=qka_psum[:, 1, :].rearrange("p (y x) -> p y x", x=SIDE)
+                out=ka_sb[:], in_=qka_psum[:, 1, :].rearrange("p (y x) -> p y x", x=SIDE)
             )
             for h in range(GROUP):
                 rows = slice(h * HEAD_DIM, (h + 1) * HEAD_DIM)
@@ -345,31 +324,52 @@ def tile_relation_s_kernel(tc, x, w_qkv, out):
                 )
 
         def a_values():
-            for s, (block, blocks, top) in enumerate(SUM_TILES):
-                mx(va_psum[:, s, :], x_mx, slice(top * SIDE, top * SIDE + P), a_mx["va"], every)
+            for s, top in enumerate(SUM_TOPS):
+                first = top * SIDE
+                scales, start = (x_scales, first) if first % (2 * SHIFT) == 0 else (x_scales_moved, first + SHIFT)
+                for g in range(PASSES):
+                    nc.tensor.matmul_mx(
+                        out=va_psum[:, s, :],
+                        lhsT=x_codes[:, g, first : first + P].bitcast(FP8X4),
+                        lhsT_scale=scales[:, g, start : start + P],
+                        rhs=w_mx["va"][0][:, g, :].bitcast(FP8X4),
+                        rhs_scale=w_mx["va"][1][:, g, :],
+                        start=(g == 0),
+                        stop=(g == PASSES - 1),
+                    )
             nc.scalar.copy(out=va_sb[:], in_=va_psum[:])
 
         s_psum = []
 
+        def rows_inside(block):
+            first = 2 * block - PAD
+            return max(0, -first), min(NB_ROWS, SIDE - first)
+
         def a_scores(first_block, last_block):
             for block in range(first_block, last_block):
+                lo, hi = rows_inside(block)
                 if block % (BLOCKS // 2) == 0:
                     s_psum.append(misc.tile([P, BLOCKS // 2, NB], F32, tag="misc", name="s_psum"))
                 nc.tensor.matmul(
-                    out=s_psum[-1][:, block % (BLOCKS // 2), :],
+                    out=s_psum[-1][:, block % (BLOCKS // 2), lo * SIDE : hi * SIDE],
                     lhsT=q_diag[:, block].rearrange("p h w -> p (h w)"),
-                    rhs=ka_pad[:, 2 * block : 2 * block + NB_ROWS, :].rearrange("p y x -> p (y x)"),
+                    rhs=ka_sb[:, 2 * block - PAD + lo : 2 * block - PAD + hi, :].rearrange("p y x -> p (y x)"),
                     start=True,
                     stop=True,
                 )
 
         def a_mask(half):
-            nc.vector.tensor_tensor(
-                out=masked[:, half * (BLOCKS // 2) : (half + 1) * (BLOCKS // 2), 0:NB],
-                in0=s_psum[half][:],
-                in1=mask[:].unsqueeze(1).to_broadcast([P, BLOCKS // 2, NB]),
-                op=ALU.add,
-            )
+            edge = 0 if half == 0 else BLOCKS - 1
+            for first_block, blocks in ((edge, 1), (1 + half * (BLOCKS // 2 - 1), BLOCKS // 2 - 1)):
+                lo, hi = rows_inside(first_block)
+                cols = slice(lo * SIDE, hi * SIDE)
+                at = first_block % (BLOCKS // 2)
+                nc.vector.tensor_tensor(
+                    out=masked[:, first_block : first_block + blocks, cols],
+                    in0=s_psum[half][:, at : at + blocks, cols],
+                    in1=mask[:, cols].unsqueeze(1).to_broadcast([P, blocks, (hi - lo) * SIDE]),
+                    op=ALU.add,
+                )
 
         def a_exp():
             nc.vector.tensor_reduce(out=top_a[:], in_=masked[:], axis=AXIS_X, op=ALU.max)
@@ -387,42 +387,30 @@ def tile_relation_s_kernel(tc, x, w_qkv, out):
 
         def a_normalise():
             nc.vector.reciprocal(out=inv_a[:], in_=total_a[:])
-            for s, (first_block, blocks, top) in enumerate(SUM_TILES):
-                for block in range(first_block, first_block + blocks):
-                    first = 2 * block - PAD
-                    lo = max(0, -first)
-                    hi = min(NB_ROWS, SIDE - first)
-                    at = first + lo - top
-                    nc.scalar.activation(
-                        out=att_a[:, block, at * SIDE : (at + hi - lo) * SIDE],
-                        in_=e_a[:, block, lo * SIDE : hi * SIDE],
-                        func=ACT.Copy,
-                        scale=inv_a[:, block : block + 1],
-                    )
-
-        def a_turn():
-            for s, (first_block, blocks, top) in enumerate(SUM_TILES):
-                turned = stream.tile([P, 3, GROUP, BLOCK_PIX], F32, tag="stream")
-                for k in range(blocks):
-                    nc.tensor.transpose(
-                        turned[:, k].rearrange("p h w -> p (h w)"), att_a[:, first_block + k, :], ident[:]
-                    )
-                nc.scalar.copy(
-                    out=att_t[:, first_block * P : (first_block + blocks) * P].rearrange(
-                        "p (h k w) -> p h k w", h=GROUP, w=BLOCK_PIX
-                    ),
-                    in_=turned[:, 0:blocks].rearrange("p k h w -> p h k w"),
+            for block in range(BLOCKS):
+                lo, hi = rows_inside(block)
+                at = 2 * block - PAD + lo - SUM_TOPS[block // SUM_BLOCKS]
+                nc.scalar.activation(
+                    out=att_a[:, block, at * SIDE : (at + hi - lo) * SIDE],
+                    in_=e_a[:, block, lo * SIDE : hi * SIDE],
+                    func=ACT.Copy,
+                    scale=inv_a[:, block : block + 1],
                 )
 
+        def a_turn(s):
+            turned = stream.tile([P, SUM_BLOCKS, GROUP, BLOCK_PIX], F32, tag="stream")
+            for k in range(SUM_BLOCKS):
+                nc.tensor.transpose(
+                    turned[:, k].rearrange("p h w -> p (h w)"), att_a[:, s * SUM_BLOCKS + k, :], ident[:]
+                )
+            nc.scalar.copy(out=att_t[:, s], in_=turned[:].rearrange("p k h w -> p h k w"))
+
         def a_sum(sum_a, s):
-            first_block, blocks, top = SUM_TILES[s]
-            for h in range(GROUP):
-                start = first_block * P + h * blocks * BLOCK_PIX
-                cols = slice(h * HEAD_DIM, (h + 1) * HEAD_DIM)
+            for q in range(PAIRS):
                 nc.tensor.matmul(
-                    out=sum_a[:, s, cols],
-                    lhsT=att_t[:, start : start + P],
-                    rhs=va_sb[:, s, cols],
+                    out=sum_a[:, s, q, :],
+                    lhsT=att_t[:, s, 2 * q : 2 * q + 2].rearrange("p h k w -> p (h k w)"),
+                    rhs=va_sb[:, s, q * 2 * HEAD_DIM : (q + 1) * 2 * HEAD_DIM],
                     start=True,
                     stop=True,
                 )
@@ -435,7 +423,7 @@ def tile_relation_s_kernel(tc, x, w_qkv, out):
             for o in range(o_first, min(o_first + 4, WIN)):
                 i, j = ROW_ORDER[o // KSIZE], o % KSIZE
                 k_window = k_pad[:, :, i : i + ROWS, j : j + SIDE]
-                qk = work.tile([P, HALVES, P], F32, bufs=10)
+                qk = work.tile([P, HALVES, P], F32, bufs=16)
                 qk_image = qk[:].rearrange("p b (y x) -> p b y x", x=SIDE)
                 if o in GPSIMD_OFFSETS:
                     nc.gpsimd.tensor_tensor(
@@ -473,40 +461,36 @@ def tile_relation_s_kernel(tc, x, w_qkv, out):
                 op=ALU.add,
             )
 
-        wt_a = {}
-        for part in ("qa", "ka", "va"):
-            wt_a[part] = transpose_weight(part, ident)
         tiles = {}
+        turn_weight("ka", to_scalar)
+        turn_weight("vb", to_scalar)
         tiles[0] = b_products(0)
-        a_group("qa")
-        a_quantise("qa")
-        tiles[4] = b_products(4)
-        a_group("ka")
-        b_reduce(0, b_turn(tiles[0]))
-        a_quantise("ka")
+        w_mx["ka"] = quantise_weight("ka", grouped["ka"])
         a_project()
+        turn_weight("va", to_scalar)
+        tiles[4] = b_products(4)
+        w_mx["vb"] = quantise_weight("vb", grouped["vb"])
+        b_values()
+        b_reduce(0, b_turn(tiles[0]))
         tiles[8] = b_products(8)
+        w_mx["va"] = quantise_weight("va", grouped["va"])
+        a_scores(0, 4)
         b_reduce(4, b_turn(tiles[4]))
-        a_group("va")
+        a_scores(4, 8)
+        a_mask(0)
         tiles[12] = b_products(12)
         b_reduce(8, b_turn(tiles[8]))
-        a_quantise("va")
-        a_scores(0, 3)
-        tiles[16] = b_products(16)
-        b_reduce(12, b_turn(tiles[12]))
-        a_scores(3, 6)
-        a_mask(0)
-        tiles[20] = b_products(20)
-        b_reduce(16, b_turn(tiles[16]))
-        a_scores(6, 8)
         a_values()
         a_mask(1)
         a_exp()
+        tiles[16] = b_products(16)
+        b_reduce(12, b_turn(tiles[12]))
+        tiles[20] = b_products(20)
+        b_reduce(16, b_turn(tiles[16]))
         tiles[24] = b_products(24)
+        a_normalise()
         b_reduce(20, b_turn(tiles[20]))
         b_reduce(24, b_turn(tiles[24]))
-        a_normalise()
-        hold_clock()
 
         top_b = keep.tile([P, rows_of_softmax], F32)
         nc.vector.tensor_reduce(out=top_b[:], in_=scores[:].rearrange("p o r -> p r o"), axis=AXIS_X, op=ALU.max)
@@ -540,9 +524,8 @@ def tile_relation_s_kernel(tc, x, w_qkv, out):
             )
 
         out_rows = out.rearrange("n c h w -> (n c) (h w)")
-        a_turn()
-        sum_a = misc.tile([P, len(SUM_TILES), P], F32, tag="misc")
-        final_a = misc.tile([P, len(SUM_TILES), P], F32, tag="misc")
+        sum_a = misc.tile([P, len(SUM_TOPS), PAIRS, 2 * HEAD_DIM], F32, tag="misc")
+        final_a = misc.tile([P, PAIRS, P], F32, tag="misc")
         results = [misc.tile([P, P], F32, tag="misc", name="result_%d" % t) for t in range(PIX_TILES)]
         out_b = keep.tile([P, PIX_TILES, P], F32)
 
@@ -582,25 +565,33 @@ def tile_relation_s_kernel(tc, x, w_qkv, out):
             nc.scalar.copy(out=out_b[:, t], in_=results[t][:])
             nc.sync.dma_start(out=out_rows[P : 2 * P, t * P : (t + 1) * P], in_=out_b[:, t])
 
+        for s in range(len(SUM_TOPS)):
+            a_turn(s)
         a_sum(sum_a, 0)
-        b_weigh(0, 0)
         a_sum(sum_a, 1)
-        b_weigh(0, 1)
+        b_weigh(0, 0)
         a_sum(sum_a, 2)
+        a_sum(sum_a, 3)
+        b_weigh(0, 1)
         b_weigh(0, 2)
-        sum_a_sb = keep.tile([P, len(SUM_TILES), P], F32)
-        nc.scalar.copy(out=sum_a_sb[:], in_=sum_a[:])
+        sum_a_sb = keep.tile([P, PAIRS, HEAD_DIM, len(SUM_TOPS)], F32)
+        for e in range(2):
+            rows = slice(e * SUM_PIX, (e + 1) * SUM_PIX)
+            nc.scalar.copy(
+                out=sum_a_sb[rows], in_=sum_a[rows, :, :, e * HEAD_DIM : (e + 1) * HEAD_DIM].rearrange("p s q c -> p q c s")
+            )
         b_weigh(0, 3)
-        for s in range(len(SUM_TILES)):
-            nc.tensor.transpose(final_a[:, s, :], sum_a_sb[:, s, :], ident[:])
+        for q in range(PAIRS):
+            nc.tensor.transpose(final_a[:, q, :], sum_a_sb[:, q].rearrange("p c s -> p (c s)"), ident[:])
         b_weigh(0, 4)
         b_weigh(1, 0)
-        out_a = keep.tile([P, PIX], F32)
-        for s, (first_block, blocks, top) in enumerate(SUM_TILES):
-            n = blocks * BLOCK_PIX
-            nc.scalar.copy(out=out_a[:, first_block * BLOCK_PIX : first_block * BLOCK_PIX + n], in_=final_a[:, s, 0:n])
+        out_a = keep.tile([P, PAIRS, P], F32)
+        nc.scalar.copy(out=out_a[:], in_=final_a[:])
         b_store(0)
         for i in range(1, KSIZE):
             b_weigh(1, i)
         b_store(1)
-        nc.sync.dma_start(out=out_rows[0:P, :], in_=out_a[:])
+        nc.sync.dma_start(
+            out=out_rows[0:P, :].rearrange("(h c) (s w) -> (c s) h w", h=GROUP, s=len(SUM_TOPS)),
+            in_=out_a[:].rearrange("p q (e w) -> p (q e) w", e=2),
+        )

@@ -46,8 +46,8 @@ PAIRS = GROUP // 2
 SHIFT = 32
 BIG = 2.0**100
 
-SCALAR_FROM = (3, 4, 3, 4, 3)
-GPSIMD_OFFSETS = tuple(range(1, WIN, 2))
+SCALAR_FROM = (4, 4, 4, 4, 4)
+GPSIMD_OFFSETS = tuple(o for o in range(WIN) if o % 3)
 ROW_ORDER = (2, 0, 1, 3, 4)
 
 FLOPS = 2 * 3 * D * C_IN * PIX + 2 * 2 * D * WIN * PIX
@@ -69,7 +69,7 @@ def tile_relation_s_kernel(tc, x, w_qkv, out):
             nc.sync.dma_start(out=x_sb[:, g].rearrange("p t w -> p (t w)"), in_=x_view[:, g, :])
         first_row = {"qa": 0, "qb": P, "ka": D, "kb": D + P, "va": 2 * D, "vb": 2 * D + P}
         w_sb = {}
-        for part in ("kb", "qb", "qa", "ka", "vb", "va"):
+        for part in ("vb", "kb", "qb", "qa", "ka", "va"):
             w_sb[part] = keep.tile([P, C_IN], BF16, name="w_sb_" + part)
             row = first_row[part]
             nc.sync.dma_start(out=w_sb[part][:], in_=w_qkv[row : row + P, :])
@@ -261,30 +261,6 @@ def tile_relation_s_kernel(tc, x, w_qkv, out):
             order = split_heads if part in split_codes else ident
             grouped[part] = group_weight(part, transpose_weight(part, order), copy_out)
 
-        turn_weight("kb", to_vector)
-        turn_weight("qb", to_scalar)
-        turn_weight("qa", to_scalar)
-        kb_mx = quantise_split_weight("kb", grouped["kb"])
-        qb_mx = quantise_split_weight("qb", grouped["qb"])
-        kb_psum = misc.tile([P, 2, HALVES, P], F32, tag="misc")
-        for b in range(HALVES):
-            mx_split(kb_psum[:, 0, b, :], kb_mx, b, 0)
-        qb_psum = hold.tile([P, HALVES, P], F32)
-        for b in range(HALVES):
-            mx_split(qb_psum[:, b, :], qb_mx, b, 0)
-        for b in range(HALVES):
-            mx_split(kb_psum[:, 1, b, :], kb_mx, b, 1)
-        w_mx["qa"] = quantise_weight("qa", grouped["qa"])
-        kb_view = kb_psum[:].rearrange("p o b (y x) -> p o b y x", x=SIDE)
-        inner = slice(PAD, PAD + SIDE)
-        qb_sb = keep.tile([P, HALVES, P], F32)
-        nc.vector.tensor_copy(out=k_pad[:, :, PAD : PAD + ROWS, inner], in_=kb_view[:, 0])
-        nc.scalar.copy(out=qb_sb[:], in_=qb_psum[:])
-        nc.scalar.copy(
-            out=k_pad[0:HALF, :, PAD + ROWS : 2 * PAD + ROWS, inner], in_=kb_view[0:HALF, 1, :, 0:PAD, :]
-        )
-        nc.scalar.copy(out=k_pad[HALF:P, :, 0:PAD, inner], in_=kb_view[HALF:P, 1, :, ROWS - PAD : ROWS, :])
-
         vb_psum = misc.tile([P, PIX_TILES, P], F32, tag="misc")
         vb_sb = keep.tile([P, PIX_TILES, P], F32)
         v_win = keep.tile([P, PIX_TILES, WIN, P], F32)
@@ -299,6 +275,45 @@ def tile_relation_s_kernel(tc, x, w_qkv, out):
                 first = P + (i - PAD) * SIDE + j - PAD
                 nc.sync.dma_start(
                     out=v_win[:, :, o, :], in_=parked[first : first + PIX, :].rearrange("(t p) c -> p t c", p=P)
+                )
+
+        turn_weight("vb", to_scalar)
+
+        turn_weight("kb", to_vector)
+        turn_weight("qb", to_scalar)
+        w_mx["vb"] = quantise_weight("vb", grouped["vb"])
+        b_values()
+        kb_mx = quantise_split_weight("kb", grouped["kb"])
+        qb_mx = quantise_split_weight("qb", grouped["qb"])
+        kb_psum = misc.tile([P, 2, HALVES, P], F32, tag="misc")
+        for b in range(HALVES):
+            mx_split(kb_psum[:, 0, b, :], kb_mx, b, 0)
+        qb_psum = hold.tile([P, HALVES, P], F32)
+        for b in range(HALVES):
+            mx_split(qb_psum[:, b, :], qb_mx, b, 0)
+        for b in range(HALVES):
+            mx_split(kb_psum[:, 1, b, :], kb_mx, b, 1)
+        kb_view = kb_psum[:].rearrange("p o b (y x) -> p o b y x", x=SIDE)
+        inner = slice(PAD, PAD + SIDE)
+        qb_sb = keep.tile([P, HALVES, P], F32)
+        nc.vector.tensor_copy(out=k_pad[:, :, PAD : PAD + ROWS, inner], in_=kb_view[:, 0])
+        nc.scalar.copy(out=qb_sb[:], in_=qb_psum[:])
+        nc.scalar.copy(
+            out=k_pad[0:HALF, :, PAD + ROWS : 2 * PAD + ROWS, inner], in_=kb_view[0:HALF, 1, :, 0:PAD, :]
+        )
+        nc.scalar.copy(out=k_pad[HALF:P, :, 0:PAD, inner], in_=kb_view[HALF:P, 1, :, ROWS - PAD : ROWS, :])
+
+        def hold_clock(passes):
+            idle = stream.tile([P, PASSES * PIX], F32, tag="stream")
+            for k in range(passes):
+                nc.tensor.matmul_mx(
+                    out=idle[:],
+                    lhsT=x_codes[:, 0, 0:P].bitcast(FP8X4),
+                    lhsT_scale=x_scales[:, 0, 0:P],
+                    rhs=x_codes[:].rearrange("p g w -> p (g w)").bitcast(FP8X4),
+                    rhs_scale=x_scales[:].rearrange("p g w -> p (g w)"),
+                    start=True,
+                    stop=True,
                 )
 
         qka_psum = misc.tile([P, 2, PIX], F32, tag="misc")
@@ -461,17 +476,16 @@ def tile_relation_s_kernel(tc, x, w_qkv, out):
                 op=ALU.add,
             )
 
-        tiles = {}
+        turn_weight("qa", to_scalar)
         turn_weight("ka", to_scalar)
-        turn_weight("vb", to_scalar)
+        tiles = {}
         tiles[0] = b_products(0)
+        w_mx["qa"] = quantise_weight("qa", grouped["qa"])
+        tiles[4] = b_products(4)
         w_mx["ka"] = quantise_weight("ka", grouped["ka"])
         a_project()
-        turn_weight("va", to_scalar)
-        tiles[4] = b_products(4)
-        w_mx["vb"] = quantise_weight("vb", grouped["vb"])
-        b_values()
         b_reduce(0, b_turn(tiles[0]))
+        turn_weight("va", to_scalar)
         tiles[8] = b_products(8)
         w_mx["va"] = quantise_weight("va", grouped["va"])
         a_scores(0, 4)
@@ -491,6 +505,7 @@ def tile_relation_s_kernel(tc, x, w_qkv, out):
         a_normalise()
         b_reduce(20, b_turn(tiles[20]))
         b_reduce(24, b_turn(tiles[24]))
+        hold_clock(2)
 
         top_b = keep.tile([P, rows_of_softmax], F32)
         nc.vector.tensor_reduce(out=top_b[:], in_=scores[:].rearrange("p o r -> p r o"), axis=AXIS_X, op=ALU.max)

@@ -47,7 +47,7 @@ SHIFT = 32
 BIG = 2.0**100
 
 SCALAR_FROM = (4, 4, 4, 4, 4)
-GPSIMD_OFFSETS = tuple(o for o in range(WIN) if o % 3)
+GPSIMD_OFFSETS = tuple(o for o in range(WIN) if o % 5 in (0, 4) and o // 5 != 4)
 ROW_ORDER = (2, 0, 1, 3, 4)
 
 FLOPS = 2 * 3 * D * C_IN * PIX + 2 * 2 * D * WIN * PIX

@@ -47,7 +47,6 @@ SHIFT = 32
 BIG = 2.0**100
 
 SCALAR_FROM = (4, 4, 4, 4, 4)
-GPSIMD_OFFSETS = tuple(o for o in range(WIN) if o % 5 in (0, 4) and o // 5 != 4)
 ROW_ORDER = (2, 0, 1, 3, 4)
 
 FLOPS = 2 * 3 * D * C_IN * PIX + 2 * 2 * D * WIN * PIX
@@ -87,21 +86,23 @@ def tile_relation_s_kernel(tc, x, w_qkv, out):
         nc.scalar.copy(
             out=q_diag[:].rearrange("p k h w -> p (k h w)"), in_=zero[:, 0:1].to_broadcast([P, BLOCKS * P])
         )
-        k_pad = keep.tile([P, HALVES, ROWS + 2 * PAD, SIDE + 2 * PAD], F32)
-        nc.vector.memset(k_pad[:], 0.0)
+        k_pad = keep.tile([P, 2, HALVES, ROWS + 2 * PAD, SIDE + 2 * PAD], F32)
+        nc.gpsimd.memset(k_pad[:], 0.0)
         split_codes = {}
         split_scales = {}
         for part in ("kb", "qb"):
             split_codes[part] = keep.tile([P, PASSES, 5 * HALF], U32, align_bytes=64, name="codes_" + part)
             split_scales[part] = keep.tile([P, PASSES, 5 * HALF], U8, align_bytes=64, name="scales_" + part)
-            nc.vector.memset(split_codes[part][:].rearrange("p g (z o) -> p g z o", o=HALF)[:, :, 0:5:2, :], 0)
-            nc.vector.memset(split_scales[part][:].rearrange("p g o -> p (g o)").bitcast(I32), 0)
+            nc.gpsimd.memset(split_codes[part][:].rearrange("p g (z o) -> p g z o", o=HALF)[:, :, 0:5:2, :], 0)
+            nc.gpsimd.memset(split_scales[part][:].rearrange("p g o -> p (g o)").bitcast(I32), 0)
         x_scales = keep.tile([P, PASSES, PIX], U8, align_bytes=64)
         nc.gpsimd.memset(x_scales[:].rearrange("p g w -> p (g w)").bitcast(I32), 0)
         column = keep.tile([P, SIDE + 2 * PAD], F32)
-        nc.gpsimd.memset(column[:], 0.0)
+        nc.vector.memset(column[:], 0.0)
         att_a = keep.tile([P, BLOCKS, P], F32)
-        nc.gpsimd.memset(att_a[:], 0.0)
+        nc.scalar.copy(
+            out=att_a[:].rearrange("p k n -> p (k n)"), in_=zero[:, 0:1].to_broadcast([P, BLOCKS * P])
+        )
         att_t = keep.tile([P, len(SUM_TOPS), GROUP, SUM_BLOCKS, BLOCK_PIX], F32)
         split_heads = keep.tile([P, P], F32)
         nc.vector.tensor_copy(
@@ -127,13 +128,13 @@ def tile_relation_s_kernel(tc, x, w_qkv, out):
             hi = PAD + SIDE - max(0, j - PAD)
             nc.vector.tensor_reduce(out=inside[:, j : j + 1], in_=column[:, lo:hi], axis=AXIS_X, op=ALU.add)
         band = keep.tile([P, KSIZE - 1, SIDE], F32)
-        nc.gpsimd.tensor_tensor(out=band[:, 0], in0=column[:, 0:SIDE], in1=column[:, 1 : 1 + SIDE], op=ALU.add)
+        nc.vector.tensor_tensor(out=band[:, 0], in0=column[:, 0:SIDE], in1=column[:, 1 : 1 + SIDE], op=ALU.add)
         for j in range(2, KSIZE):
-            nc.gpsimd.tensor_tensor(out=band[:, j - 1], in0=band[:, j - 2], in1=column[:, j : j + SIDE], op=ALU.add)
+            nc.vector.tensor_tensor(out=band[:, j - 1], in0=band[:, j - 2], in1=column[:, j : j + SIDE], op=ALU.add)
         in_window = keep.tile([P, NB_ROWS, SIDE], F32)
         for rows, pick in ((slice(0, 1), row_of_two[:, 0:1]), (slice(1, 5), 1.0), (slice(5, 6), row_of_two[:, 1:2])):
             n = rows.stop - rows.start
-            nc.gpsimd.tensor_scalar(
+            nc.vector.tensor_scalar(
                 out=in_window[:, rows],
                 in0=band[:, KSIZE - 2].unsqueeze(1).to_broadcast([P, n, SIDE]),
                 scalar1=pick,
@@ -142,7 +143,7 @@ def tile_relation_s_kernel(tc, x, w_qkv, out):
                 op1=ALU.add,
             )
         mask = keep.tile([P, NB], F32)
-        nc.gpsimd.tensor_scalar(
+        nc.vector.tensor_scalar(
             out=mask[:],
             in0=in_window[:].rearrange("p r x -> p (r x)"),
             scalar1=1.0,
@@ -150,21 +151,6 @@ def tile_relation_s_kernel(tc, x, w_qkv, out):
             op0=ALU.subtract,
             op1=ALU.mult,
         )
-        masked = keep.tile([P, BLOCKS, COLS], F32)
-        for block, cols in ((0, slice(0, PAD * SIDE)), (BLOCKS - 1, slice(NB - PAD * SIDE, NB))):
-            nc.gpsimd.tensor_copy(out=masked[:, block, cols], in_=mask[:, cols])
-        beside = keep.tile([P, 2], F32)
-        nc.gpsimd.tensor_tensor(out=beside[:, 0:1], in0=inside[:, 0:1], in1=inside[:, 4:5], op=ALU.add)
-        nc.gpsimd.tensor_tensor(out=beside[:, 1:2], in0=inside[:, 1:2], in1=inside[:, 3:4], op=ALU.add)
-        for f in range(2):
-            nc.gpsimd.tensor_scalar(
-                out=masked[:, :, NB + f * KSIZE : NB + (f + 1) * KSIZE],
-                in0=beside[:, f : f + 1].unsqueeze(1).to_broadcast([P, BLOCKS, KSIZE]),
-                scalar1=-BIG,
-                scalar2=BIG,
-                op0=ALU.mult,
-                op1=ALU.add,
-            )
 
         x_grouped = keep.tile([P, PASSES, PIX, PACK], BF16, align_bytes=64)
         x_codes = keep.tile([P, PASSES, PIX], U32, align_bytes=64)
@@ -178,13 +164,6 @@ def tile_relation_s_kernel(tc, x, w_qkv, out):
                 in_=x_grouped[:, g].rearrange("p w t -> p (w t)"),
             )
         x_mx = (x_codes, x_scales)
-        words = PIX // 4
-        nc.gpsimd.tensor_copy(
-            out=x_scales_moved[:].rearrange("p g w -> p (g w)").bitcast(I32).rearrange("p (g w) -> p g w", g=PASSES)[
-                :, :, SHIFT // 4 : SHIFT // 4 + words
-            ],
-            in_=x_scales[:].rearrange("p g w -> p (g w)").bitcast(I32).rearrange("p (g w) -> p g w", g=PASSES),
-        )
 
         def transpose_weight(part, order):
             words = w_sb[part][:].bitcast(F32)
@@ -285,23 +264,48 @@ def tile_relation_s_kernel(tc, x, w_qkv, out):
         b_values()
         kb_mx = quantise_split_weight("kb", grouped["kb"])
         qb_mx = quantise_split_weight("qb", grouped["qb"])
-        kb_psum = misc.tile([P, 2, HALVES, P], F32, tag="misc")
+        masked = keep.tile([P, BLOCKS, COLS], F32)
+        for block, cols in ((0, slice(0, PAD * SIDE)), (BLOCKS - 1, slice(NB - PAD * SIDE, NB))):
+            nc.vector.tensor_copy(out=masked[:, block, cols], in_=mask[:, cols])
+        beside = keep.tile([P, 2], F32)
+        nc.vector.tensor_tensor(out=beside[:, 0:1], in0=inside[:, 0:1], in1=inside[:, 4:5], op=ALU.add)
+        nc.vector.tensor_tensor(out=beside[:, 1:2], in0=inside[:, 1:2], in1=inside[:, 3:4], op=ALU.add)
+        for f in range(2):
+            nc.vector.tensor_scalar(
+                out=masked[:, :, NB + f * KSIZE : NB + (f + 1) * KSIZE],
+                in0=beside[:, f : f + 1].unsqueeze(1).to_broadcast([P, BLOCKS, KSIZE]),
+                scalar1=-BIG,
+                scalar2=BIG,
+                op0=ALU.mult,
+                op1=ALU.add,
+            )
+        words = PIX // 4
+        nc.vector.tensor_copy(
+            out=x_scales_moved[:].rearrange("p g w -> p (g w)").bitcast(I32).rearrange("p (g w) -> p g w", g=PASSES)[
+                :, :, SHIFT // 4 : SHIFT // 4 + words
+            ],
+            in_=x_scales[:].rearrange("p g w -> p (g w)").bitcast(I32).rearrange("p (g w) -> p g w", g=PASSES),
+        )
+        kb_psum = misc.tile([P, HALVES, P], F32, tag="misc")
         for b in range(HALVES):
-            mx_split(kb_psum[:, 0, b, :], kb_mx, b, 0)
+            mx_split(kb_psum[:, b, :], kb_mx, b, 0)
         qb_psum = hold.tile([P, HALVES, P], F32)
         for b in range(HALVES):
             mx_split(qb_psum[:, b, :], qb_mx, b, 0)
+        halo_psum = misc.tile([P, HALVES, P], F32, tag="misc")
         for b in range(HALVES):
-            mx_split(kb_psum[:, 1, b, :], kb_mx, b, 1)
-        kb_view = kb_psum[:].rearrange("p o b (y x) -> p o b y x", x=SIDE)
-        inner = slice(PAD, PAD + SIDE)
-        qb_sb = keep.tile([P, HALVES, P], F32)
-        nc.vector.tensor_copy(out=k_pad[:, :, PAD : PAD + ROWS, inner], in_=kb_view[:, 0])
-        nc.scalar.copy(out=qb_sb[:], in_=qb_psum[:])
-        nc.scalar.copy(
-            out=k_pad[0:HALF, :, PAD + ROWS : 2 * PAD + ROWS, inner], in_=kb_view[0:HALF, 1, :, 0:PAD, :]
-        )
-        nc.scalar.copy(out=k_pad[HALF:P, :, 0:PAD, inner], in_=kb_view[HALF:P, 1, :, ROWS - PAD : ROWS, :])
+            mx_split(halo_psum[:, b, :], kb_mx, b, 1)
+        kb_view = kb_psum[:].rearrange("p b (y x) -> p b y x", x=SIDE)
+        halo_view = halo_psum[:].rearrange("p b (y x) -> p b y x", x=SIDE)
+        for s, copy_out in ((0, nc.vector.tensor_copy), (1, nc.scalar.copy)):
+            inner = slice(PAD - s, PAD - s + SIDE)
+            copy_out(out=k_pad[:, s, :, PAD : PAD + ROWS, inner], in_=kb_view)
+        for s in range(2):
+            inner = slice(PAD - s, PAD - s + SIDE)
+            nc.scalar.copy(
+                out=k_pad[0:HALF, s, :, PAD + ROWS : 2 * PAD + ROWS, inner], in_=halo_view[0:HALF, :, 0:PAD, :]
+            )
+            nc.scalar.copy(out=k_pad[HALF:P, s, :, 0:PAD, inner], in_=halo_view[HALF:P, :, ROWS - PAD : ROWS, :])
 
         def hold_clock(passes):
             idle = stream.tile([P, PASSES * PIX], F32, tag="stream")
@@ -433,33 +437,32 @@ def tile_relation_s_kernel(tc, x, w_qkv, out):
         rows_of_softmax = PIX_TILES * GROUP
         scores = keep.tile([P, WIN, rows_of_softmax], F32)
 
-        def b_products(o_first):
-            tiles = []
-            for o in range(o_first, min(o_first + 4, WIN)):
-                i, j = ROW_ORDER[o // KSIZE], o % KSIZE
-                k_window = k_pad[:, :, i : i + ROWS, j : j + SIDE]
-                qk = work.tile([P, HALVES, P], F32, bufs=16)
-                qk_image = qk[:].rearrange("p b (y x) -> p b y x", x=SIDE)
-                if o in GPSIMD_OFFSETS:
-                    nc.gpsimd.tensor_tensor(
-                        out=qk_image, in0=qb_sb[:].rearrange("p b (y x) -> p b y x", x=SIDE), in1=k_window, op=ALU.mult
-                    )
-                else:
-                    nc.vector.tensor_tensor(
-                        out=qk_image, in0=qb_psum[:].rearrange("p b (y x) -> p b y x", x=SIDE), in1=k_window, op=ALU.mult
-                    )
-                tiles.append((o, qk))
-            return tiles
+        products = {}
 
-        def b_turn(tiles):
+        def b_products(row):
+            i = ROW_ORDER[row]
+            for j in (4, 0, 2):
+                n = min(2, KSIZE - j)
+                qk = work.tile([P, 2, HALVES, P], F32, bufs=9)
+                nc.vector.tensor_tensor(
+                    out=qk[:, 0:n].rearrange("p s b (y x) -> p s b y x", x=SIDE),
+                    in0=qb_psum[:]
+                    .rearrange("p b (y x) -> p b y x", x=SIDE)
+                    .unsqueeze(1)
+                    .to_broadcast([P, n, HALVES, ROWS, SIDE]),
+                    in1=k_pad[:, 0:n, :, i : i + ROWS, j : j + SIDE],
+                    op=ALU.mult,
+                )
+                for s in range(n):
+                    products[row * KSIZE + j + s] = qk[:, s]
+
+        def b_turn(o_first):
             halves = stream.tile([P, 4, P], F32, tag="stream")
-            for o, qk in [pair for pair in tiles if pair[0] not in GPSIMD_OFFSETS] + [
-                pair for pair in tiles if pair[0] in GPSIMD_OFFSETS
-            ]:
+            for o in range(o_first, min(o_first + 4, WIN)):
                 for b in range(HALVES):
                     nc.tensor.matmul(
-                        out=halves[:, o - tiles[0][0], :],
-                        lhsT=qk[:, b, :],
+                        out=halves[:, o - o_first, :],
+                        lhsT=products[o][:, b, :],
                         rhs=ident[:],
                         is_transpose=True,
                         start=(b == 0),
@@ -478,33 +481,31 @@ def tile_relation_s_kernel(tc, x, w_qkv, out):
 
         turn_weight("qa", to_scalar)
         turn_weight("ka", to_scalar)
-        tiles = {}
-        tiles[0] = b_products(0)
+        b_products(0)
         w_mx["qa"] = quantise_weight("qa", grouped["qa"])
-        tiles[4] = b_products(4)
+        b_products(1)
         w_mx["ka"] = quantise_weight("ka", grouped["ka"])
+        halves = b_turn(0)
         a_project()
-        b_reduce(0, b_turn(tiles[0]))
+        b_reduce(0, halves)
         turn_weight("va", to_scalar)
-        tiles[8] = b_products(8)
+        b_products(2)
+        b_reduce(4, b_turn(4))
         w_mx["va"] = quantise_weight("va", grouped["va"])
         a_scores(0, 4)
-        b_reduce(4, b_turn(tiles[4]))
+        b_products(3)
+        b_reduce(8, b_turn(8))
         a_scores(4, 8)
         a_mask(0)
-        tiles[12] = b_products(12)
-        b_reduce(8, b_turn(tiles[8]))
-        a_values()
+        b_reduce(12, b_turn(12))
         a_mask(1)
         a_exp()
-        tiles[16] = b_products(16)
-        b_reduce(12, b_turn(tiles[12]))
-        tiles[20] = b_products(20)
-        b_reduce(16, b_turn(tiles[16]))
-        tiles[24] = b_products(24)
+        a_values()
+        b_products(4)
         a_normalise()
-        b_reduce(20, b_turn(tiles[20]))
-        b_reduce(24, b_turn(tiles[24]))
+        b_reduce(16, b_turn(16))
+        b_reduce(20, b_turn(20))
+        b_reduce(24, b_turn(24))
         hold_clock(2)
 
         top_b = keep.tile([P, rows_of_softmax], F32)
@@ -603,10 +604,10 @@ def tile_relation_s_kernel(tc, x, w_qkv, out):
         out_a = keep.tile([P, PAIRS, P], F32)
         nc.scalar.copy(out=out_a[:], in_=final_a[:])
         b_store(0)
-        for i in range(1, KSIZE):
-            b_weigh(1, i)
-        b_store(1)
         nc.sync.dma_start(
             out=out_rows[0:P, :].rearrange("(h c) (s w) -> (c s) h w", h=GROUP, s=len(SUM_TOPS)),
             in_=out_a[:].rearrange("p q (e w) -> p (q e) w", e=2),
         )
+        for i in range(1, KSIZE):
+            b_weigh(1, i)
+        b_store(1)

@@ -258,7 +258,7 @@ def tile_relation_s_kernel(tc, x, w_qkv, out):
 
         turn_weight("vb", to_scalar)
 
-        turn_weight("kb", to_vector)
+        turn_weight("kb", to_scalar)
         turn_weight("qb", to_scalar)
         w_mx["vb"] = quantise_weight("vb", grouped["vb"])
         b_values()
@@ -297,6 +297,8 @@ def tile_relation_s_kernel(tc, x, w_qkv, out):
             mx_split(halo_psum[:, b, :], kb_mx, b, 1)
         kb_view = kb_psum[:].rearrange("p b (y x) -> p b y x", x=SIDE)
         halo_view = halo_psum[:].rearrange("p b (y x) -> p b y x", x=SIDE)
+        qb_sb = keep.tile([P, HALVES, P], F32)
+        nc.scalar.copy(out=qb_sb[:], in_=qb_psum[:])
         for s, copy_out in ((0, nc.vector.tensor_copy), (1, nc.scalar.copy)):
             inner = slice(PAD - s, PAD - s + SIDE)
             copy_out(out=k_pad[:, s, :, PAD : PAD + ROWS, inner], in_=kb_view)
@@ -306,19 +308,6 @@ def tile_relation_s_kernel(tc, x, w_qkv, out):
                 out=k_pad[0:HALF, s, :, PAD + ROWS : 2 * PAD + ROWS, inner], in_=halo_view[0:HALF, :, 0:PAD, :]
             )
             nc.scalar.copy(out=k_pad[HALF:P, s, :, 0:PAD, inner], in_=halo_view[HALF:P, :, ROWS - PAD : ROWS, :])
-
-        def hold_clock(passes):
-            idle = stream.tile([P, PASSES * PIX], F32, tag="stream")
-            for k in range(passes):
-                nc.tensor.matmul_mx(
-                    out=idle[:],
-                    lhsT=x_codes[:, 0, 0:P].bitcast(FP8X4),
-                    lhsT_scale=x_scales[:, 0, 0:P],
-                    rhs=x_codes[:].rearrange("p g w -> p (g w)").bitcast(FP8X4),
-                    rhs_scale=x_scales[:].rearrange("p g w -> p (g w)"),
-                    start=True,
-                    stop=True,
-                )
 
         qka_psum = misc.tile([P, 2, PIX], F32, tag="misc")
         va_psum = misc.tile([P, len(SUM_TOPS), P], F32, tag="misc")
@@ -390,12 +379,13 @@ def tile_relation_s_kernel(tc, x, w_qkv, out):
                     op=ALU.add,
                 )
 
-        def a_exp():
-            nc.vector.tensor_reduce(out=top_a[:], in_=masked[:], axis=AXIS_X, op=ALU.max)
+        def a_exp(half):
+            blocks = slice(half * (BLOCKS // 2), (half + 1) * (BLOCKS // 2))
+            nc.vector.tensor_reduce(out=top_a[:, blocks], in_=masked[:, blocks], axis=AXIS_X, op=ALU.max)
             nc.vector.tensor_scalar(
-                out=minus_top[:], in0=top_a[:], scalar1=-1.0, scalar2=0.0, op0=ALU.mult, op1=ALU.add
+                out=minus_top[:, blocks], in0=top_a[:, blocks], scalar1=-1.0, scalar2=0.0, op0=ALU.mult, op1=ALU.add
             )
-            for block in range(BLOCKS):
+            for block in range(blocks.start, blocks.stop):
                 nc.scalar.activation(
                     out=e_a[:, block],
                     in_=masked[:, block],
@@ -404,9 +394,10 @@ def tile_relation_s_kernel(tc, x, w_qkv, out):
                     accum_out=total_a[:, block : block + 1],
                 )
 
-        def a_normalise():
-            nc.vector.reciprocal(out=inv_a[:], in_=total_a[:])
-            for block in range(BLOCKS):
+        def a_normalise(half):
+            blocks = slice(half * (BLOCKS // 2), (half + 1) * (BLOCKS // 2))
+            nc.vector.reciprocal(out=inv_a[:, blocks], in_=total_a[:, blocks])
+            for block in range(blocks.start, blocks.stop):
                 lo, hi = rows_inside(block)
                 at = 2 * block - PAD + lo - SUM_TOPS[block // SUM_BLOCKS]
                 nc.scalar.activation(
@@ -441,8 +432,18 @@ def tile_relation_s_kernel(tc, x, w_qkv, out):
 
         def b_products(row):
             i = ROW_ORDER[row]
-            for j in (4, 0, 2):
-                n = min(2, KSIZE - j)
+            shared = row < KSIZE - 1
+            if shared:
+                for j in (0, KSIZE - 1):
+                    qk = work.tile([P, HALVES, P], F32, bufs=9, name="qk_shared")
+                    nc.gpsimd.tensor_tensor(
+                        out=qk[:].rearrange("p b (y x) -> p b y x", x=SIDE),
+                        in0=qb_sb[:].rearrange("p b (y x) -> p b y x", x=SIDE),
+                        in1=k_pad[:, 0, :, i : i + ROWS, j : j + SIDE],
+                        op=ALU.mult,
+                    )
+                    products[row * KSIZE + j] = qk
+            for j, n in ((3, 1), (1, 2)) if shared else ((4, 1), (0, 2), (2, 2)):
                 qk = work.tile([P, 2, HALVES, P], F32, bufs=9)
                 nc.vector.tensor_tensor(
                     out=qk[:, 0:n].rearrange("p s b (y x) -> p s b y x", x=SIDE),
@@ -495,18 +496,26 @@ def tile_relation_s_kernel(tc, x, w_qkv, out):
         a_scores(0, 4)
         b_products(3)
         b_reduce(8, b_turn(8))
-        a_scores(4, 8)
         a_mask(0)
+        a_exp(0)
+        a_scores(4, 8)
         b_reduce(12, b_turn(12))
-        a_mask(1)
-        a_exp()
         a_values()
+        a_normalise(0)
+        a_mask(1)
+        a_exp(1)
         b_products(4)
-        a_normalise()
+        for s in range(2):
+            a_turn(s)
         b_reduce(16, b_turn(16))
+        a_normalise(1)
+        sum_a = misc.tile([P, len(SUM_TOPS), PAIRS, 2 * HEAD_DIM], F32, tag="misc")
         b_reduce(20, b_turn(20))
         b_reduce(24, b_turn(24))
-        hold_clock(2)
+        for s in range(2):
+            a_sum(sum_a, s)
+        for s in range(2, 4):
+            a_turn(s)
 
         top_b = keep.tile([P, rows_of_softmax], F32)
         nc.vector.tensor_reduce(out=top_b[:], in_=scores[:].rearrange("p o r -> p r o"), axis=AXIS_X, op=ALU.max)
@@ -540,7 +549,6 @@ def tile_relation_s_kernel(tc, x, w_qkv, out):
             )
 
         out_rows = out.rearrange("n c h w -> (n c) (h w)")
-        sum_a = misc.tile([P, len(SUM_TOPS), PAIRS, 2 * HEAD_DIM], F32, tag="misc")
         final_a = misc.tile([P, PAIRS, P], F32, tag="misc")
         results = [misc.tile([P, P], F32, tag="misc", name="result_%d" % t) for t in range(PIX_TILES)]
         out_b = keep.tile([P, PIX_TILES, P], F32)
@@ -581,13 +589,9 @@ def tile_relation_s_kernel(tc, x, w_qkv, out):
             nc.scalar.copy(out=out_b[:, t], in_=results[t][:])
             nc.sync.dma_start(out=out_rows[P : 2 * P, t * P : (t + 1) * P], in_=out_b[:, t])
 
-        for s in range(len(SUM_TOPS)):
-            a_turn(s)
-        a_sum(sum_a, 0)
-        a_sum(sum_a, 1)
+        for s in range(2, 4):
+            a_sum(sum_a, s)
         b_weigh(0, 0)
-        a_sum(sum_a, 2)
-        a_sum(sum_a, 3)
         b_weigh(0, 1)
         b_weigh(0, 2)
         sum_a_sb = keep.tile([P, PAIRS, HEAD_DIM, len(SUM_TOPS)], F32)

from contextlib import ExitStack

import concourse.mybir as mybir
from concourse.masks import make_identity

F32 = mybir.dt.float32
BF16 = mybir.dt.bfloat16
U32 = mybir.dt.uint32
I32 = mybir.dt.int32
U8 = mybir.dt.uint8
FP8X4 = mybir.dt.float8_e4m3fn_x4
ALU = mybir.AluOpType
ACT = mybir.ActivationFunctionType
AXIS_X = mybir.AxisListType.X
AXIS_XY = mybir.AxisListType.XY

P = 128
PACK = 4
C_IN = 1024
PASSES = C_IN // (P * PACK)
D = 256
HEADS = 8
HEAD_DIM = D // HEADS
SIDE = 16
PIX = SIDE * SIDE
KSIZE = 5
PAD = KSIZE // 2
WIN = KSIZE * KSIZE
PIX_TILES = PIX // P
ROWS = P // SIDE
GROUP = 4
HALVES = 2
HALF_HEAD = HEAD_DIM // HALVES
HALF = GROUP * HALF_HEAD

BLOCKS = 8
BLOCK_PIX = PIX // BLOCKS
NB_ROWS = 2 + 2 * PAD
NB = NB_ROWS * SIDE
BESIDE = 2 * KSIZE
COLS = NB + BESIDE
SUM_TOPS = (0, 2, 6, 8)
SUM_BLOCKS = BLOCKS // len(SUM_TOPS)
SUM_PIX = SUM_BLOCKS * BLOCK_PIX
PAIRS = GROUP // 2
SHIFT = 32
BIG = 2.0**100

SCALAR_FROM = (4, 4, 4, 4, 4)
ROW_ORDER = (2, 0, 1, 3, 4)

FLOPS = 2 * 3 * D * C_IN * PIX + 2 * 2 * D * WIN * PIX


def tile_relation_s_kernel(tc, x, w_qkv, out):
    nc = tc.nc
    with ExitStack() as ctx:
        keep = ctx.enter_context(tc.tile_pool(name="keep", bufs=1))
        work = ctx.enter_context(tc.tile_pool(name="work", bufs=4))
        stream = ctx.enter_context(tc.psum_pool(name="stream", bufs=3))
        misc = ctx.enter_context(tc.psum_pool(name="misc", bufs=4))
        hold = ctx.enter_context(tc.psum_pool(name="hold", bufs=1))
        ctx.enter_context(tc.manual_schedule())

        x_sb = keep.tile([P, PASSES, PACK, PIX], BF16)
        x_view = x.rearrange("n (g q t) h w -> q (n g) (t h w)", g=PASSES, q=P, t=PACK)
        for g in range(PASSES):
            nc.sync.dma_start(out=x_sb[:, g].rearrange("p t w -> p (t w)"), in_=x_view[:, g, :])
        first_row = {"qa": 0, "qb": P, "ka": D, "kb": D + P, "va": 2 * D, "vb": 2 * D + P}
        w_sb = {}
        for part in ("vb", "kb", "qb", "qa", "ka", "va"):
            w_sb[part] = keep.tile([P, C_IN], BF16, name="w_sb_" + part)
            row = first_row[part]
            nc.sync.dma_start(out=w_sb[part][:], in_=w_qkv[row : row + P, :])

        ident = keep.tile([P, P], F32)
        make_identity(nc, ident[:])
        zero = keep.tile([P, P], F32)
        nc.vector.memset(zero[:], 0.0)
        warm_out = keep.tile([P, 1], F32)
        nc.scalar.activation(out=warm_out[:], in_=zero[:, 0:1], func=ACT.Exp)
        parked = out.rearrange("n c h w -> (n c) (h w)").rearrange("r (s c) -> (r s) c", s=2)
        nc.scalar.dma_start(out=parked[0:P, :], in_=zero[:])
        nc.scalar.dma_start(out=parked[3 * P : 4 * P, :], in_=zero[:])
        q_diag = keep.tile([P, BLOCKS, GROUP, BLOCK_PIX], F32)
        nc.scalar.copy(
            out=q_diag[:].rearrange("p k h w -> p (k h w)"), in_=zero[:, 0:1].to_broadcast([P, BLOCKS * P])
        )
        k_pad = keep.tile([P, 2, HALVES, ROWS + 2 * PAD, SIDE + 2 * PAD], F32)
        nc.gpsimd.memset(k_pad[:], 0.0)
        split_codes = {}
        split_scales = {}
        for part in ("kb", "qb"):
            split_codes[part] = keep.tile([P, PASSES, 5 * HALF], U32, align_bytes=64, name="codes_" + part)
            split_scales[part] = keep.tile([P, PASSES, 5 * HALF], U8, align_bytes=64, name="scales_" + part)
            nc.gpsimd.memset(split_codes[part][:].rearrange("p g (z o) -> p g z o", o=HALF)[:, :, 0:5:2, :], 0)
            nc.gpsimd.memset(split_scales[part][:].rearrange("p g o -> p (g o)").bitcast(I32), 0)
        x_scales = keep.tile([P, PASSES, PIX], U8, align_bytes=64)
        nc.gpsimd.memset(x_scales[:].rearrange("p g w -> p (g w)").bitcast(I32), 0)
        column = keep.tile([P, SIDE + 2 * PAD], F32)
        nc.vector.memset(column[:], 0.0)
        att_a = keep.tile([P, BLOCKS, P], F32)
        nc.scalar.copy(
            out=att_a[:].rearrange("p k n -> p (k n)"), in_=zero[:, 0:1].to_broadcast([P, BLOCKS * P])
        )
        att_t = keep.tile([P, len(SUM_TOPS), GROUP, SUM_BLOCKS, BLOCK_PIX], F32)
        split_heads = keep.tile([P, P], F32)
        nc.vector.tensor_copy(
            out=split_heads[:].rearrange("p (b h c) -> p b h c", b=HALVES, c=HALF_HEAD),
            in_=ident[:].rearrange("p (h b c) -> p b h c", b=HALVES, c=HALF_HEAD),
        )
        nc.vector.tensor_reduce(
            out=column[:, PAD : PAD + SIDE],
            in_=ident[:].rearrange("p (y x) -> p x y", x=SIDE),
            axis=AXIS_X,
            op=ALU.add,
        )
        row_of_two = keep.tile([P, 2], F32)
        nc.vector.tensor_reduce(
            out=row_of_two[:],
            in_=ident[:].rearrange("p (y r x) -> p r y x", r=2, x=SIDE),
            axis=AXIS_XY,
            op=ALU.add,
        )
        inside = keep.tile([P, KSIZE], F32)
        for j in range(KSIZE):
            lo = PAD + max(0, PAD - j)
            hi = PAD + SIDE - max(0, j - PAD)
            nc.vector.tensor_reduce(out=inside[:, j : j + 1], in_=column[:, lo:hi], axis=AXIS_X, op=ALU.add)
        band = keep.tile([P, KSIZE - 1, SIDE], F32)
        nc.vector.tensor_tensor(out=band[:, 0], in0=column[:, 0:SIDE], in1=column[:, 1 : 1 + SIDE], op=ALU.add)
        for j in range(2, KSIZE):
            nc.vector.tensor_tensor(out=band[:, j - 1], in0=band[:, j - 2], in1=column[:, j : j + SIDE], op=ALU.add)
        in_window = keep.tile([P, NB_ROWS, SIDE], F32)
        for rows, pick in ((slice(0, 1), row_of_two[:, 0:1]), (slice(1, 5), 1.0), (slice(5, 6), row_of_two[:, 1:2])):
            n = rows.stop - rows.start
            nc.vector.tensor_scalar(
                out=in_window[:, rows],
                in0=band[:, KSIZE - 2].unsqueeze(1).to_broadcast([P, n, SIDE]),
                scalar1=pick,
                scalar2=0.0,
                op0=ALU.mult,
                op1=ALU.add,
            )
        mask = keep.tile([P, NB], F32)
        nc.vector.tensor_scalar(
            out=mask[:],
            in0=in_window[:].rearrange("p r x -> p (r x)"),
            scalar1=1.0,
            scalar2=BIG,
            op0=ALU.subtract,
            op1=ALU.mult,
        )

        x_grouped = keep.tile([P, PASSES, PIX, PACK], BF16, align_bytes=64)
        x_codes = keep.tile([P, PASSES, PIX], U32, align_bytes=64)
        x_scales_moved = keep.tile([P, PASSES, PIX + 2 * SHIFT], U8, align_bytes=64)
        for g in range(PASSES):
            nc.vector.tensor_copy(out=x_grouped[:, g], in_=x_sb[:, g].rearrange("p t w -> p w t"))
        for g in range(PASSES):
            nc.vector.quantize_mx(
                out=x_codes[:, g].bitcast(FP8X4),
                scales=x_scales[:, g],
                in_=x_grouped[:, g].rearrange("p w t -> p (w t)"),
            )
        x_mx = (x_codes, x_scales)

        def transpose_weight(part, order):
            words = w_sb[part][:].bitcast(F32)
            wt = stream.tile([P, PASSES, 2, P], F32, tag="stream", name="wt_" + part)
            for g in range(PASSES):
                for u in range(2):
                    nc.tensor.transpose(wt[:, g, u, :], words[:, 2 * P * g + u : 2 * P * (g + 1) : 2], order[:])
            return wt

        def group_weight(part, wt, copy_out):
            grouped = keep.tile([P, PASSES, P, PACK], BF16, align_bytes=64, name="grouped_" + part)
            copy_out(
                out=grouped[:].rearrange("p g o t -> p (g o t)").bitcast(F32).rearrange("p (g o u) -> p g o u", g=PASSES, u=2),
                in_=wt[:].rearrange("p g u o -> p g o u"),
            )
            return grouped

        def quantise_weight(part, grouped):
            codes = keep.tile([P, PASSES, P], U32, align_bytes=64, name="codes_" + part)
            scales = keep.tile([P, PASSES, P], U8, align_bytes=64, name="scales_" + part)
            nc.vector.quantize_mx(
                out=codes[:].rearrange("p g o -> p (g o)").bitcast(FP8X4),
                scales=scales[:].rearrange("p g o -> p (g o)"),
                in_=grouped[:].rearrange("p g o t -> p (g o t)"),
            )
            return codes, scales

        def quantise_split_weight(part, grouped):
            for g in range(PASSES):
                for b in range(HALVES):
                    to = slice(HALF + 2 * HALF * b, 2 * HALF + 2 * HALF * b)
                    nc.vector.quantize_mx(
                        out=split_codes[part][:, g, to].bitcast(FP8X4),
                        scales=split_scales[part][:, g, to],
                        in_=grouped[:, g, b * HALF : (b + 1) * HALF, :].rearrange("p o t -> p (o t)"),
                    )
            return split_codes[part], split_scales[part]

        def mx(out_ap, lhs, lhs_cols, rhs, rhs_cols, first=True, last=True):
            for g in range(PASSES):
                nc.tensor.matmul_mx(
                    out=out_ap,
                    lhsT=lhs[0][:, g, lhs_cols].bitcast(FP8X4),
                    lhsT_scale=lhs[1][:, g, lhs_cols],
                    rhs=rhs[0][:, g, rhs_cols].bitcast(FP8X4),
                    rhs_scale=rhs[1][:, g, rhs_cols],
                    start=(first and g == 0),
                    stop=(last and g == PASSES - 1),
                )

        def mx_split(out_ap, part, b, other):
            for t in range(PIX_TILES):
                start = HALF + 2 * HALF * b - HALF * t
                tile = (t + other) % PIX_TILES
                mx(
                    out_ap,
                    part,
                    slice(start, start + P),
                    x_mx,
                    slice(tile * P, (tile + 1) * P),
                    first=(t == 0),
                    last=(t == PIX_TILES - 1),
                )

        every = slice(0, P)
        all_pix = slice(0, PIX)
        to_vector = nc.vector.tensor_copy
        to_scalar = nc.scalar.copy

        grouped = {}
        w_mx = {}

        def turn_weight(part, copy_out):
            order = split_heads if part in split_codes else ident
            grouped[part] = group_weight(part, transpose_weight(part, order), copy_out)

        vb_psum = misc.tile([P, PIX_TILES, P], F32, tag="misc")
        vb_sb = keep.tile([P, PIX_TILES, P], F32)
        v_win = keep.tile([P, PIX_TILES, WIN, P], F32)

        def b_values():
            for t in range(PIX_TILES):
                mx(vb_psum[:, t, :], x_mx, slice(t * P, (t + 1) * P), w_mx["vb"], every)
            nc.scalar.copy(out=vb_sb[:], in_=vb_psum[:])
            nc.sync.dma_start(out=parked[P : 3 * P, :].rearrange("(t p) c -> p t c", p=P), in_=vb_sb[:])
            for o in range(WIN):
                i, j = ROW_ORDER[o // KSIZE], o % KSIZE
                first = P + (i - PAD) * SIDE + j - PAD
                nc.sync.dma_start(
                    out=v_win[:, :, o, :], in_=parked[first : first + PIX, :].rearrange("(t p) c -> p t c", p=P)
                )

        turn_weight("vb", to_scalar)

        turn_weight("kb", to_scalar)
        turn_weight("qb", to_scalar)
        w_mx["vb"] = quantise_weight("vb", grouped["vb"])
        b_values()
        kb_mx = quantise_split_weight("kb", grouped["kb"])
        qb_mx = quantise_split_weight("qb", grouped["qb"])
        masked = keep.tile([P, BLOCKS, COLS], F32)
        for block, cols in ((0, slice(0, PAD * SIDE)), (BLOCKS - 1, slice(NB - PAD * SIDE, NB))):
            nc.vector.tensor_copy(out=masked[:, block, cols], in_=mask[:, cols])
        beside = keep.tile([P, 2], F32)
        nc.vector.tensor_tensor(out=beside[:, 0:1], in0=inside[:, 0:1], in1=inside[:, 4:5], op=ALU.add)
        nc.vector.tensor_tensor(out=beside[:, 1:2], in0=inside[:, 1:2], in1=inside[:, 3:4], op=ALU.add)
        for f in range(2):
            nc.vector.tensor_scalar(
                out=masked[:, :, NB + f * KSIZE : NB + (f + 1) * KSIZE],
                in0=beside[:, f : f + 1].unsqueeze(1).to_broadcast([P, BLOCKS, KSIZE]),
                scalar1=-BIG,
                scalar2=BIG,
                op0=ALU.mult,
                op1=ALU.add,
            )
        words = PIX // 4
        nc.vector.tensor_copy(
            out=x_scales_moved[:].rearrange("p g w -> p (g w)").bitcast(I32).rearrange("p (g w) -> p g w", g=PASSES)[
                :, :, SHIFT // 4 : SHIFT // 4 + words
            ],
            in_=x_scales[:].rearrange("p g w -> p (g w)").bitcast(I32).rearrange("p (g w) -> p g w", g=PASSES),
        )
        kb_psum = misc.tile([P, HALVES, P], F32, tag="misc")
        for b in range(HALVES):
            mx_split(kb_psum[:, b, :], kb_mx, b, 0)
        qb_psum = hold.tile([P, HALVES, P], F32)
        for b in range(HALVES):
            mx_split(qb_psum[:, b, :], qb_mx, b, 0)
        halo_psum = misc.tile([P, HALVES, P], F32, tag="misc")
        for b in range(HALVES):
            mx_split(halo_psum[:, b, :], kb_mx, b, 1)
        kb_view = kb_psum[:].rearrange("p b (y x) -> p b y x", x=SIDE)
        halo_view = halo_psum[:].rearrange("p b (y x) -> p b y x", x=SIDE)
        qb_sb = keep.tile([P, HALVES, P], F32)
        nc.scalar.copy(out=qb_sb[:], in_=qb_psum[:])
        for s, copy_out in ((0, nc.vector.tensor_copy), (1, nc.scalar.copy)):
            inner = slice(PAD - s, PAD - s + SIDE)
            copy_out(out=k_pad[:, s, :, PAD : PAD + ROWS, inner], in_=kb_view)
        for s in range(2):
            inner = slice(PAD - s, PAD - s + SIDE)
            nc.scalar.copy(
                out=k_pad[0:HALF, s, :, PAD + ROWS : 2 * PAD + ROWS, inner], in_=halo_view[0:HALF, :, 0:PAD, :]
            )
            nc.scalar.copy(out=k_pad[HALF:P, s, :, 0:PAD, inner], in_=halo_view[HALF:P, :, ROWS - PAD : ROWS, :])

        qka_psum = misc.tile([P, 2, PIX], F32, tag="misc")
        va_psum = misc.tile([P, len(SUM_TOPS), P], F32, tag="misc")
        va_sb = keep.tile([P, len(SUM_TOPS), P], F32)
        ka_sb = keep.tile([P, SIDE, SIDE], F32)
        top_a = keep.tile([P, BLOCKS], F32)
        minus_top = keep.tile([P, BLOCKS], F32)
        e_a = keep.tile([P, BLOCKS, COLS], F32)
        total_a = keep.tile([P, BLOCKS], F32)
        inv_a = keep.tile([P, BLOCKS], F32)

        def a_project():
            mx(qka_psum[:, 0, :], w_mx["qa"], every, x_mx, all_pix)
            mx(qka_psum[:, 1, :], w_mx["ka"], every, x_mx, all_pix)
            nc.scalar.copy(
                out=ka_sb[:], in_=qka_psum[:, 1, :].rearrange("p (y x) -> p y x", x=SIDE)
            )
            for h in range(GROUP):
                rows = slice(h * HEAD_DIM, (h + 1) * HEAD_DIM)
                nc.scalar.copy(
                    out=q_diag[rows, :, h, :], in_=qka_psum[rows, 0, :].rearrange("p (k w) -> p k w", k=BLOCKS)
                )

        def a_values():
            for s, top in enumerate(SUM_TOPS):
                first = top * SIDE
                scales, start = (x_scales, first) if first % (2 * SHIFT) == 0 else (x_scales_moved, first + SHIFT)
                for g in range(PASSES):
                    nc.tensor.matmul_mx(
                        out=va_psum[:, s, :],
                        lhsT=x_codes[:, g, first : first + P].bitcast(FP8X4),
                        lhsT_scale=scales[:, g, start : start + P],
                        rhs=w_mx["va"][0][:, g, :].bitcast(FP8X4),
                        rhs_scale=w_mx["va"][1][:, g, :],
                        start=(g == 0),
                        stop=(g == PASSES - 1),
                    )
            nc.scalar.copy(out=va_sb[:], in_=va_psum[:])

        s_psum = []

        def rows_inside(block):
            first = 2 * block - PAD
            return max(0, -first), min(NB_ROWS, SIDE - first)

        def a_scores(first_block, last_block):
            for block in range(first_block, last_block):
                lo, hi = rows_inside(block)
                if block % (BLOCKS // 2) == 0:
                    s_psum.append(misc.tile([P, BLOCKS // 2, NB], F32, tag="misc", name="s_psum"))
                nc.tensor.matmul(
                    out=s_psum[-1][:, block % (BLOCKS // 2), lo * SIDE : hi * SIDE],
                    lhsT=q_diag[:, block].rearrange("p h w -> p (h w)"),
                    rhs=ka_sb[:, 2 * block - PAD + lo : 2 * block - PAD + hi, :].rearrange("p y x -> p (y x)"),
                    start=True,
                    stop=True,
                )

        def a_mask(half):
            edge = 0 if half == 0 else BLOCKS - 1
            for first_block, blocks in ((edge, 1), (1 + half * (BLOCKS // 2 - 1), BLOCKS // 2 - 1)):
                lo, hi = rows_inside(first_block)
                cols = slice(lo * SIDE, hi * SIDE)
                at = first_block % (BLOCKS // 2)
                nc.vector.tensor_tensor(
                    out=masked[:, first_block : first_block + blocks, cols],
                    in0=s_psum[half][:, at : at + blocks, cols],
                    in1=mask[:, cols].unsqueeze(1).to_broadcast([P, blocks, (hi - lo) * SIDE]),
                    op=ALU.add,
                )

        def a_exp(half):
            blocks = slice(half * (BLOCKS // 2), (half + 1) * (BLOCKS // 2))
            nc.vector.tensor_reduce(out=top_a[:, blocks], in_=masked[:, blocks], axis=AXIS_X, op=ALU.max)
            nc.vector.tensor_scalar(
                out=minus_top[:, blocks], in0=top_a[:, blocks], scalar1=-1.0, scalar2=0.0, op0=ALU.mult, op1=ALU.add
            )
            for block in range(blocks.start, blocks.stop):
                nc.scalar.activation(
                    out=e_a[:, block],
                    in_=masked[:, block],
                    func=ACT.Exp,
                    bias=minus_top[:, block : block + 1],
                    accum_out=total_a[:, block : block + 1],
                )

        def a_normalise(half):
            blocks = slice(half * (BLOCKS // 2), (half + 1) * (BLOCKS // 2))
            nc.vector.reciprocal(out=inv_a[:, blocks], in_=total_a[:, blocks])
            for block in range(blocks.start, blocks.stop):
                lo, hi = rows_inside(block)
                at = 2 * block - PAD + lo - SUM_TOPS[block // SUM_BLOCKS]
                nc.scalar.activation(
                    out=att_a[:, block, at * SIDE : (at + hi - lo) * SIDE],
                    in_=e_a[:, block, lo * SIDE : hi * SIDE],
                    func=ACT.Copy,
                    scale=inv_a[:, block : block + 1],
                )

        def a_turn(s):
            turned = stream.tile([P, SUM_BLOCKS, GROUP, BLOCK_PIX], F32, tag="stream")
            for k in range(SUM_BLOCKS):
                nc.tensor.transpose(
                    turned[:, k].rearrange("p h w -> p (h w)"), att_a[:, s * SUM_BLOCKS + k, :], ident[:]
                )
            nc.scalar.copy(out=att_t[:, s], in_=turned[:].rearrange("p k h w -> p h k w"))

        def a_sum(sum_a, s):
            for q in range(PAIRS):
                nc.tensor.matmul(
                    out=sum_a[:, s, q, :],
                    lhsT=att_t[:, s, 2 * q : 2 * q + 2].rearrange("p h k w -> p (h k w)"),
                    rhs=va_sb[:, s, q * 2 * HEAD_DIM : (q + 1) * 2 * HEAD_DIM],
                    start=True,
                    stop=True,
                )

        rows_of_softmax = PIX_TILES * GROUP
        scores = keep.tile([P, WIN, rows_of_softmax], F32)

        products = {}

        def b_products(row):
            i = ROW_ORDER[row]
            shared = row < KSIZE - 1
            if shared:
                for j in (0, KSIZE - 1):
                    qk = work.tile([P, HALVES, P], F32, bufs=9, name="qk_shared")
                    nc.gpsimd.tensor_tensor(
                        out=qk[:].rearrange("p b (y x) -> p b y x", x=SIDE),
                        in0=qb_sb[:].rearrange("p b (y x) -> p b y x", x=SIDE),
                        in1=k_pad[:, 0, :, i : i + ROWS, j : j + SIDE],
                        op=ALU.mult,
                    )
                    products[row * KSIZE + j] = qk
            for j, n in ((3, 1), (1, 2)) if shared else ((4, 1), (0, 2), (2, 2)):
                qk = work.tile([P, 2, HALVES, P], F32, bufs=9)
                nc.vector.tensor_tensor(
                    out=qk[:, 0:n].rearrange("p s b (y x) -> p s b y x", x=SIDE),
                    in0=qb_psum[:]
                    .rearrange("p b (y x) -> p b y x", x=SIDE)
                    .unsqueeze(1)
                    .to_broadcast([P, n, HALVES, ROWS, SIDE]),
                    in1=k_pad[:, 0:n, :, i : i + ROWS, j : j + SIDE],
                    op=ALU.mult,
                )
                for s in range(n):
                    products[row * KSIZE + j + s] = qk[:, s]

        def b_turn(o_first):
            halves = stream.tile([P, 4, P], F32, tag="stream")
            for o in range(o_first, min(o_first + 4, WIN)):
                for b in range(HALVES):
                    nc.tensor.matmul(
                        out=halves[:, o - o_first, :],
                        lhsT=products[o][:, b, :],
                        rhs=ident[:],
                        is_transpose=True,
                        start=(b == 0),
                        stop=(b == HALVES - 1),
                    )
            return halves

        def b_reduce(o_first, halves):
            n = min(4, WIN - o_first)
            nc.vector.tensor_reduce(
                out=scores[:, o_first : o_first + n, :].rearrange("p o r -> p (o r)"),
                in_=halves[:, 0:n].rearrange("p o (r c) -> p (o r) c", c=HALF_HEAD),
                axis=AXIS_X,
                op=ALU.add,
            )

        turn_weight("qa", to_scalar)
        turn_weight("ka", to_scalar)
        b_products(0)
        w_mx["qa"] = quantise_weight("qa", grouped["qa"])
        b_products(1)
        w_mx["ka"] = quantise_weight("ka", grouped["ka"])
        halves = b_turn(0)
        a_project()
        b_reduce(0, halves)
        turn_weight("va", to_scalar)
        b_products(2)
        b_reduce(4, b_turn(4))
        w_mx["va"] = quantise_weight("va", grouped["va"])
        a_scores(0, 4)
        b_products(3)
        b_reduce(8, b_turn(8))
        a_mask(0)
        a_exp(0)
        a_scores(4, 8)
        b_reduce(12, b_turn(12))
        a_values()
        a_normalise(0)
        a_mask(1)
        a_exp(1)
        b_products(4)
        for s in range(2):
            a_turn(s)
        b_reduce(16, b_turn(16))
        a_normalise(1)
        sum_a = misc.tile([P, len(SUM_TOPS), PAIRS, 2 * HEAD_DIM], F32, tag="misc")
        b_reduce(20, b_turn(20))
        b_reduce(24, b_turn(24))
        for s in range(2):
            a_sum(sum_a, s)
        for s in range(2, 4):
            a_turn(s)

        top_b = keep.tile([P, rows_of_softmax], F32)
        nc.vector.tensor_reduce(out=top_b[:], in_=scores[:].rearrange("p o r -> p r o"), axis=AXIS_X, op=ALU.max)
        centred = keep.tile([P, WIN, rows_of_softmax], F32)
        nc.vector.tensor_tensor(
            out=centred[:],
            in0=scores[:],
            in1=top_b[:].unsqueeze(1).to_broadcast([P, WIN, rows_of_softmax]),
            op=ALU.subtract,
        )
        e_b = keep.tile([P, WIN, rows_of_softmax], F32)
        nc.scalar.activation(out=e_b[:], in_=centred[:], func=ACT.Exp)
        total_b = keep.tile([P, rows_of_softmax], F32)
        nc.vector.tensor_reduce(out=total_b[:], in_=e_b[:].rearrange("p o r -> p r o"), axis=AXIS_X, op=ALU.add)
        inv_b = keep.tile([P, rows_of_softmax], F32)
        nc.vector.reciprocal(out=inv_b[:], in_=total_b[:])
        inv_inside = keep.tile([P, KSIZE, rows_of_softmax], F32)
        nc.vector.tensor_tensor(
            out=inv_inside[:],
            in0=inv_b[:].unsqueeze(1).to_broadcast([P, KSIZE, rows_of_softmax]),
            in1=inside[:].unsqueeze(2).to_broadcast([P, KSIZE, rows_of_softmax]),
            op=ALU.mult,
        )
        att_b = keep.tile([P, PIX_TILES, WIN, GROUP], F32)
        for t in range(PIX_TILES):
            nc.vector.tensor_tensor(
                out=att_b[:, t].rearrange("p (i j) h -> p i j h", j=KSIZE),
                in0=e_b[:, :, t * GROUP : (t + 1) * GROUP].rearrange("p (i j) h -> p i j h", j=KSIZE),
                in1=inv_inside[:, :, t * GROUP : (t + 1) * GROUP].unsqueeze(1).to_broadcast([P, KSIZE, KSIZE, GROUP]),
                op=ALU.mult,
            )

        out_rows = out.rearrange("n c h w -> (n c) (h w)")
        final_a = misc.tile([P, PAIRS, P], F32, tag="misc")
        results = [misc.tile([P, P], F32, tag="misc", name="result_%d" % t) for t in range(PIX_TILES)]
        out_b = keep.tile([P, PIX_TILES, P], F32)

        def b_weigh(t, i):
            av = work.tile([P, KSIZE, P], F32)
            split = SCALAR_FROM[i]
            o = i * KSIZE
            nc.vector.tensor_tensor(
                out=av[:, 0:split].rearrange("p o (h c) -> p (o h) c", h=GROUP),
                in0=v_win[:, t, o : o + split, :].rearrange("p o (h c) -> p (o h) c", h=GROUP),
                in1=att_b[:, t, o : o + split, :]
                .rearrange("p o h -> p (o h)")
                .unsqueeze(2)
                .to_broadcast([P, split * GROUP, HEAD_DIM]),
                op=ALU.mult,
            )
            for j in range(split, KSIZE):
                for h in range(GROUP):
                    cols = slice(h * HEAD_DIM, (h + 1) * HEAD_DIM)
                    nc.scalar.activation(
                        out=av[:, j, cols],
                        in_=v_win[:, t, o + j, cols],
                        func=ACT.Copy,
                        scale=att_b[:, t, o + j, h : h + 1],
                    )
            for j in range(KSIZE):
                nc.tensor.matmul(
                    out=results[t][:],
                    lhsT=av[:, j, :],
                    rhs=ident[:],
                    is_transpose=True,
                    start=(o + j == 0),
                    stop=(o + j == WIN - 1),
                )

        def b_store(t):
            nc.scalar.copy(out=out_b[:, t], in_=results[t][:])
            nc.sync.dma_start(out=out_rows[P : 2 * P, t * P : (t + 1) * P], in_=out_b[:, t])

        for s in range(2, 4):
            a_sum(sum_a, s)
        b_weigh(0, 0)
        b_weigh(0, 1)
        b_weigh(0, 2)
        sum_a_sb = keep.tile([P, PAIRS, HEAD_DIM, len(SUM_TOPS)], F32)
        for e in range(2):
            rows = slice(e * SUM_PIX, (e + 1) * SUM_PIX)
            nc.scalar.copy(
                out=sum_a_sb[rows], in_=sum_a[rows, :, :, e * HEAD_DIM : (e + 1) * HEAD_DIM].rearrange("p s q c -> p q c s")
            )
        b_weigh(0, 3)
        for q in range(PAIRS):
            nc.tensor.transpose(final_a[:, q, :], sum_a_sb[:, q].rearrange("p c s -> p (c s)"), ident[:])
        b_weigh(0, 4)
        b_weigh(1, 0)
        out_a = keep.tile([P, PAIRS, P], F32)
        nc.scalar.copy(out=out_a[:], in_=final_a[:])
        b_store(0)
        nc.sync.dma_start(
            out=out_rows[0:P, :].rearrange("(h c) (s w) -> (c s) h w", h=GROUP, s=len(SUM_TOPS)),
            in_=out_a[:].rearrange("p q (e w) -> p (q e) w", e=2),
        )
        for i in range(1, KSIZE):
            b_weigh(1, i)
        b_store(1)
